import numpy as np
import ml_dtypes


def mxq(x, axis, fmt="e4m3"):
    dtype, down = {"e4m3": (ml_dtypes.float8_e4m3fn, 7), "e5m2": (ml_dtypes.float8_e5m2, 14)}[fmt]
    v = np.moveaxis(np.asarray(x, np.float32).astype(ml_dtypes.bfloat16).astype(np.float64), axis, -1)
    blocks = v.reshape(v.shape[:-1] + (-1, 32))
    amax = np.abs(blocks).max(-1, keepdims=True)
    byte = np.maximum(np.where(amax > 0, np.frexp(amax)[1] - 1 + 127, 0) - down, 1)
    scale = np.exp2(byte - 127.0)
    codes = (blocks / scale).astype(np.float32).astype(dtype).astype(np.float64)
    return np.moveaxis((codes * scale).reshape(v.shape), -1, axis)


WIDE = False


def mx_kscale(k):
    if not WIDE:
        return np.ones(k)
    levels = np.array([20, -20, 10, -10, 0])
    a = np.random.permutation(np.resize(levels, k // 512 * 4)).reshape(k // 512, 4)
    idx = np.arange(k)
    return np.exp2(a[idx // 512, idx % 128 // 32])


BF16 = ml_dtypes.bfloat16


def bf(x):
    return np.asarray(x, np.float32).astype(BF16)


def f64(x):
    return np.asarray(x).astype(np.float64)


B, P, L, FI, FO = 32, 2, 3, 128, 8192
C = (L + 1) * (L + 1)


def setup_inputs():
    u = mx_kscale(FO)
    x = np.random.standard_normal((B, P, C, FI))
    W_e = np.random.standard_normal((L + 1, FI, FO)) / np.sqrt(FI) / u
    W_o = np.random.standard_normal((L + 1, FI, FO)) / np.sqrt(FI) / u
    b = np.random.standard_normal(FO) * 0.5
    g = np.random.standard_normal((B, P, C, FO)) * np.exp2(np.random.randint(-12, 1, (B, P, C, 1))) * 16.0 * u
    return {"x": bf(x), "W_e": bf(W_e), "W_o": bf(W_o), "b": bf(b), "grad_out": bf(g)}


def reference(x, W_e, W_o, b, grad_out):
    gq = mxq(f64(grad_out), 3, "e5m2")
    weq = mxq(f64(W_e), 2, "e4m3")
    woq = mxq(f64(W_o), 2, "e4m3")
    gs_e, gs_o = [], []
    for l in range(L + 1):
        seg = gq[:, :, l * l:(l + 1) * (l + 1), :]
        gs_e.append(seg[:, 0] @ weq[l].T)
        gs_o.append(seg[:, 1] @ woq[l].T)
    return np.stack([np.concatenate(gs_e, axis=-2), np.concatenate(gs_o, axis=-2)], axis=-3)

@@ -1,0 +1,202 @@
+from contextlib import ExitStack
+
+import concourse.mybir as mybir
+from concourse.masks import make_identity
+
+F32 = mybir.dt.float32
+BF16 = mybir.dt.bfloat16
+U32 = mybir.dt.uint32
+U8 = mybir.dt.uint8
+E4M3_X4 = mybir.dt.float8_e4m3fn_x4
+E5M2_X4 = mybir.dt.float8_e5m2_x4
+
+ITEMS, PARITIES, COMPONENTS, DEGREES = 32, 2, 16, 4
+F_IN, F_OUT = 128, 8192
+
+P = 128
+K_PASS = 4 * P
+PASSES = F_OUT // K_PASS
+CHUNK = 2048
+CHUNKS = F_OUT // CHUNK
+CHUNK_PASSES = CHUNK // K_PASS
+ROW_TILES = ITEMS * COMPONENTS // P
+N_MOVING = DEGREES * F_IN
+QUADRANT = 32
+
+RAW_BUFS = 12
+
+FLOPS = 2 * ITEMS * PARITIES * COMPONENTS * F_IN * F_OUT
+BYTES = 2 * (ITEMS * PARITIES * COMPONENTS + PARITIES * DEGREES * F_IN) * F_OUT + 4 * ITEMS * PARITIES * COMPONENTS * F_IN
+
+
+def degree_of(component):
+    return sum(1 for l in range(1, DEGREES) if component >= l * l)
+
+
+def tile_dense_pa_k_kernel(tc, x, W_e, W_o, b, grad_out, out):
+    nc = tc.nc
+    with ExitStack() as ctx:
+        const = ctx.enter_context(tc.tile_pool(name="const", bufs=1))
+        raw_pool = ctx.enter_context(tc.tile_pool(name="raw", bufs=RAW_BUFS))
+        grouped_pool = ctx.enter_context(tc.tile_pool(name="grouped", bufs=3))
+        weight_pool = ctx.enter_context(tc.tile_pool(name="weight_codes", bufs=2))
+        even_pool = ctx.enter_context(tc.tile_pool(name="even_codes", bufs=3))
+        result_pool = ctx.enter_context(tc.tile_pool(name="result", bufs=2))
+        bank_pool = ctx.enter_context(tc.psum_pool(name="banks", bufs=CHUNK_PASSES))
+        sum_pool = ctx.enter_context(tc.psum_pool(name="sums", bufs=1))
+        ctx.enter_context(tc.manual_schedule())
+
+        grad_rows = grad_out.flatten_outer_dims().rearrange("(q h r) k -> r q h k", h=2, r=ROW_TILES)
+        weight_rows = [W.rearrange("(a l) f k -> a f l k", l=2) for W in (W_e, W_o)]
+
+        identity = const.tile([P, P], F32, name="identity")
+        make_identity(nc, identity[:])
+        sorter = const.tile([P, P], F32, name="sorter")
+        nc.vector.tensor_copy(
+            out=sorter[:].rearrange("i (p x n) -> i p x n", p=PARITIES, x=2),
+            in_=identity[:].rearrange("i (n p x) -> i p x n", p=PARITIES, x=2),
+        )
+
+        odd_codes = const.tile([P, ROW_TILES, PASSES * P], U32, name="odd_codes", align_bytes=64)
+        odd_scales = const.tile([P, ROW_TILES, PASSES * P], U8, name="odd_scales", align_bytes=64)
+
+        rounds = []
+        for chunk in range(CHUNKS):
+            for pair in range(2):
+                rounds.append({"grads": False, "parity": 0, "chunk": chunk, "pair": pair})
+            for r in range(ROW_TILES):
+                rounds.append({"grads": True, "chunk": chunk, "r": r})
+        for chunk in range(CHUNKS):
+            for pair in range(2):
+                rounds.append({"grads": False, "parity": 1, "chunk": chunk, "pair": pair})
+
+        weights = {}
+        sums = {}
+
+        def load(rnd):
+            k_cols = slice(rnd["chunk"] * CHUNK, (rnd["chunk"] + 1) * CHUNK)
+            raw = raw_pool.tile([P, 2, CHUNK], BF16, name="raw")
+            if rnd["grads"]:
+                nc.sync.dma_start(out=raw[:], in_=grad_rows[rnd["r"]][:, :, k_cols])
+            else:
+                nc.sync.dma_start(out=raw[:], in_=weight_rows[rnd["parity"]][rnd["pair"]][:, :, k_cols])
+            rnd["raw"] = raw
+
+        def copy_out(bank_index, dst, src):
+            if bank_index == 0:
+                nc.vector.tensor_copy(out=dst, in_=src)
+            else:
+                nc.scalar.copy(out=dst, in_=src)
+
+        def transpose(rnd):
+            grouped = grouped_pool.tile([P, 2 * CHUNK], BF16, name="grouped", align_bytes=64)
+            words = grouped[:].bitcast(F32)
+            for g in range(CHUNK_PASSES):
+                bank = bank_pool.tile([P, 2, 2, P], F32, name="bank")
+                for half in range(2):
+                    raw_words = rnd["raw"][:, half, :].bitcast(F32)
+                    for u in range(2):
+                        first = (2 * g + u) * P
+                        nc.tensor.transpose(
+                            bank[:, half, u, :],
+                            raw_words[:, first : first + P],
+                            sorter[:] if rnd["grads"] else identity[:],
+                        )
+                if rnd["grads"]:
+                    view = words.rearrange("w (p g h c u) -> w p g h c u", p=PARITIES, g=CHUNK_PASSES, h=2, u=2)
+                    for parity in range(PARITIES):
+                        columns = slice(parity * P // 2, (parity + 1) * P // 2)
+                        copy_out(g, view[:, parity, g], bank[:, :, :, columns].rearrange("w h u c -> w h c u"))
+                else:
+                    view = words.rearrange("w (g l f u) -> w g l f u", g=CHUNK_PASSES, l=2, u=2)
+                    copy_out(g, view[:, g], bank[:].rearrange("w l u f -> w l f u"))
+            rnd["grouped"] = grouped
+
+        def quantise(rnd):
+            grouped = rnd["grouped"]
+            if rnd["grads"]:
+                even_codes = even_pool.tile([P, CHUNK_PASSES * P], U32, name="even_codes", align_bytes=64)
+                even_scales = even_pool.tile([P, CHUNK_PASSES * P], U8, name="even_scales", align_bytes=64)
+                nc.vector.quantize_mx(out=even_codes[:].bitcast(E5M2_X4), scales=even_scales[:], in_=grouped[:, 0:CHUNK])
+                kept = slice(rnd["chunk"] * CHUNK_PASSES * P, (rnd["chunk"] + 1) * CHUNK_PASSES * P)
+                nc.vector.quantize_mx(
+                    out=odd_codes[:, rnd["r"], kept].bitcast(E5M2_X4),
+                    scales=odd_scales[:, rnd["r"], kept],
+                    in_=grouped[:, CHUNK : 2 * CHUNK],
+                )
+                rnd["even"] = (even_codes, even_scales)
+            else:
+                key = (rnd["parity"], rnd["chunk"])
+                if rnd["pair"] == 0:
+                    weight_codes = weight_pool.tile([P, CHUNK_PASSES, N_MOVING], U32, name="weight_codes", align_bytes=64)
+                    weight_scales = weight_pool.tile([P, CHUNK_PASSES, N_MOVING], U8, name="weight_scales", align_bytes=64)
+                    weights[key] = (weight_codes, weight_scales)
+                weight_codes, weight_scales = weights[key]
+                columns = slice(rnd["pair"] * 2 * F_IN, (rnd["pair"] + 1) * 2 * F_IN)
+                width = 2 * CHUNK // CHUNK_PASSES
+                for g in range(CHUNK_PASSES):
+                    nc.vector.quantize_mx(
+                        out=weight_codes[:, g, columns].bitcast(E4M3_X4),
+                        scales=weight_scales[:, g, columns],
+                        in_=grouped[:, g * width : (g + 1) * width],
+                    )
+
+        def passes(parity, r, chunk, grad_codes, grad_scales):
+            weight_codes, weight_scales = weights[(parity, chunk)]
+            if chunk == 0:
+                sums[(parity, r)] = sum_pool.tile([P, N_MOVING], F32, name="sum%d" % r)
+            for g in range(CHUNK_PASSES):
+                rows = slice(g * P, (g + 1) * P)
+                nc.tensor.matmul_mx(
+                    out=sums[(parity, r)][:],
+                    lhsT=grad_codes[:, rows].bitcast(E5M2_X4),
+                    lhsT_scale=grad_scales[:, rows],
+                    rhs=weight_codes[:, g, :].bitcast(E4M3_X4),
+                    rhs_scale=weight_scales[:, g, :],
+                    start=(chunk == 0 and g == 0),
+                    stop=(chunk == CHUNKS - 1 and g == CHUNK_PASSES - 1),
+                )
+
+        def store(parity):
+            result = result_pool.tile([P, ROW_TILES, F_IN], F32, name="result")
+            for r in range(ROW_TILES):
+                for quadrant in range(4):
+                    rows = slice(quadrant * QUADRANT, (quadrant + 1) * QUADRANT)
+                    degree = degree_of(8 * (quadrant % 2) + 4 * (quadrant // 2) + r)
+                    kept = sums[(parity, r)][rows, degree * F_IN : (degree + 1) * F_IN]
+                    if quadrant % 2 == 0:
+                        nc.vector.tensor_copy(out=result[rows, r, :], in_=kept)
+                    else:
+                        nc.scalar.copy(out=result[rows, r, :], in_=kept)
+            for quadrant in range(4):
+                rows = slice(quadrant * QUADRANT, (quadrant + 1) * QUADRANT)
+                first = 8 * (quadrant % 2) + 4 * (quadrant // 2)
+                nc.sync.dma_start(
+                    out=out[:, parity, first : first + ROW_TILES, :].rearrange("n c f -> n (c f)"),
+                    in_=result[rows, :, :].rearrange("n r f -> n (r f)"),
+                )
+
+        def multiply(rnd):
+            chunk = rnd["chunk"]
+            if rnd["grads"]:
+                passes(0, rnd["r"], chunk, rnd["even"][0], rnd["even"][1])
+                if chunk == CHUNKS - 1 and rnd["r"] == ROW_TILES - 1:
+                    store(0)
+            elif rnd["parity"] == 1 and rnd["pair"] == 1:
+                kept = slice(chunk * CHUNK_PASSES * P, (chunk + 1) * CHUNK_PASSES * P)
+                for r in range(ROW_TILES):
+                    passes(1, r, chunk, odd_codes[:, r, kept], odd_scales[:, r, kept])
+                if chunk == CHUNKS - 1:
+                    store(1)
+
+        for rnd in rounds[:RAW_BUFS]:
+            load(rnd)
+        for step in range(len(rounds) + 2):
+            if step < len(rounds):
+                transpose(rounds[step])
+            if step + RAW_BUFS < len(rounds):
+                load(rounds[step + RAW_BUFS])
+            if 0 <= step - 1 < len(rounds):
+                quantise(rounds[step - 1])
+            if step - 2 >= 0:
+                multiply(rounds[step - 2])

@@ -11,6 +11,7 @@ E4M3_X4 = mybir.dt.float8_e4m3fn_x4
 E5M2_X4 = mybir.dt.float8_e5m2_x4
 
 ITEMS, PARITIES, COMPONENTS, DEGREES = 32, 2, 16, 4
+EVEN, ODD = 0, 1
 F_IN, F_OUT = 128, 8192
 
 P = 128
@@ -22,8 +23,8 @@ CHUNK_PASSES = CHUNK // K_PASS
 ROW_TILES = ITEMS * COMPONENTS // P
 N_MOVING = DEGREES * F_IN
 QUADRANT = 32
-
-RAW_BUFS = 12
+ROUND_BANKS = 4
+ROUND_COLUMNS = 4 * ROUND_BANKS * 2 * P
 
 FLOPS = 2 * ITEMS * PARITIES * COMPONENTS * F_IN * F_OUT
 BYTES = 2 * (ITEMS * PARITIES * COMPONENTS + PARITIES * DEGREES * F_IN) * F_OUT + 4 * ITEMS * PARITIES * COMPONENTS * F_IN
@@ -37,17 +38,18 @@ def tile_dense_pa_k_kernel(tc, x, W_e, W_o, b, grad_out, out):
     nc = tc.nc
     with ExitStack() as ctx:
         const = ctx.enter_context(tc.tile_pool(name="const", bufs=1))
-        raw_pool = ctx.enter_context(tc.tile_pool(name="raw", bufs=RAW_BUFS))
+        raw_weight_pool = ctx.enter_context(tc.tile_pool(name="raw_weights", bufs=3))
+        raw_grad_pool = ctx.enter_context(tc.tile_pool(name="raw_grads", bufs=8))
         grouped_pool = ctx.enter_context(tc.tile_pool(name="grouped", bufs=3))
-        weight_pool = ctx.enter_context(tc.tile_pool(name="weight_codes", bufs=2))
+        weight_pool = ctx.enter_context(tc.tile_pool(name="weight_codes", bufs=5))
         even_pool = ctx.enter_context(tc.tile_pool(name="even_codes", bufs=3))
         result_pool = ctx.enter_context(tc.tile_pool(name="result", bufs=2))
-        bank_pool = ctx.enter_context(tc.psum_pool(name="banks", bufs=CHUNK_PASSES))
+        bank_pool = ctx.enter_context(tc.psum_pool(name="banks", bufs=ROUND_BANKS))
         sum_pool = ctx.enter_context(tc.psum_pool(name="sums", bufs=1))
         ctx.enter_context(tc.manual_schedule())
 
         grad_rows = grad_out.flatten_outer_dims().rearrange("(q h r) k -> r q h k", h=2, r=ROW_TILES)
-        weight_rows = [W.rearrange("(a l) f k -> a f l k", l=2) for W in (W_e, W_o)]
+        weight_rows = [W.rearrange("l f k -> f l k") for W in (W_e, W_o)]
 
         identity = const.tile([P, P], F32, name="identity")
         make_identity(nc, identity[:])
@@ -60,27 +62,36 @@ def tile_dense_pa_k_kernel(tc, x, W_e, W_o, b, grad_out, out):
         odd_codes = const.tile([P, ROW_TILES, PASSES * P], U32, name="odd_codes", align_bytes=64)
         odd_scales = const.tile([P, ROW_TILES, PASSES * P], U8, name="odd_scales", align_bytes=64)
 
-        rounds = []
+        def weight_round(parity, chunk, half):
+            return {"grads": False, "parity": parity, "chunk": chunk, "half": half}
+
+        rounds = [weight_round(EVEN, 0, 0), weight_round(EVEN, 0, 1)]
         for chunk in range(CHUNKS):
-            for pair in range(2):
-                rounds.append({"grads": False, "parity": 0, "chunk": chunk, "pair": pair})
             for r in range(ROW_TILES):
                 rounds.append({"grads": True, "chunk": chunk, "r": r})
+                if r % 2 == 0 and chunk + 1 < CHUNKS:
+                    rounds.append(weight_round(EVEN, chunk + 1, r // 2))
         for chunk in range(CHUNKS):
-            for pair in range(2):
-                rounds.append({"grads": False, "parity": 1, "chunk": chunk, "pair": pair})
+            for half in range(2):
+                rounds.append(weight_round(ODD, chunk, half))
 
-        weights = {}
-        sums = {}
-
-        def load(rnd):
+        raw_weights = {}
+        for rnd in rounds:
             k_cols = slice(rnd["chunk"] * CHUNK, (rnd["chunk"] + 1) * CHUNK)
-            raw = raw_pool.tile([P, 2, CHUNK], BF16, name="raw")
             if rnd["grads"]:
-                nc.sync.dma_start(out=raw[:], in_=grad_rows[rnd["r"]][:, :, k_cols])
+                raw_grads = raw_grad_pool.tile([P, 2, CHUNK], BF16, name="raw_grads")
+                nc.sync.dma_start(out=raw_grads[:], in_=grad_rows[rnd["r"]][:, :, k_cols])
+                rnd["raw"] = raw_grads
             else:
-                nc.sync.dma_start(out=raw[:], in_=weight_rows[rnd["parity"]][rnd["pair"]][:, :, k_cols])
-            rnd["raw"] = raw
+                if rnd["half"] == 0:
+                    raw_weight = raw_weight_pool.tile([P, DEGREES, CHUNK], BF16, name="raw_weight")
+                    nc.sync.dma_start(out=raw_weight[:], in_=weight_rows[rnd["parity"]][:, :, k_cols])
+                    raw_weights[(rnd["parity"], rnd["chunk"])] = raw_weight
+                rnd["raw"] = raw_weights[(rnd["parity"], rnd["chunk"])]
+
+        weight_codes = {}
+        sums = {}
+        results = {}
 
         def copy_out(bank_index, dst, src):
             if bank_index == 0:
@@ -89,113 +100,116 @@ def tile_dense_pa_k_kernel(tc, x, W_e, W_o, b, grad_out, out):
                 nc.scalar.copy(out=dst, in_=src)
 
         def transpose(rnd):
-            grouped = grouped_pool.tile([P, 2 * CHUNK], BF16, name="grouped", align_bytes=64)
+            grouped = grouped_pool.tile([P, ROUND_COLUMNS], BF16, name="grouped", align_bytes=64)
             words = grouped[:].bitcast(F32)
-            for g in range(CHUNK_PASSES):
-                bank = bank_pool.tile([P, 2, 2, P], F32, name="bank")
-                for half in range(2):
-                    raw_words = rnd["raw"][:, half, :].bitcast(F32)
-                    for u in range(2):
-                        first = (2 * g + u) * P
-                        nc.tensor.transpose(
-                            bank[:, half, u, :],
-                            raw_words[:, first : first + P],
-                            sorter[:] if rnd["grads"] else identity[:],
-                        )
+            for bank_index in range(ROUND_BANKS):
                 if rnd["grads"]:
+                    g = bank_index
+                    bank = bank_pool.tile([P, PARITIES, 2, 2, P // 2], F32, name="grad_bank", tag="bank")
+                    for h in range(2):
+                        raw_words = rnd["raw"][:, h, :].bitcast(F32)
+                        for u in range(2):
+                            first = (2 * g + u) * P
+                            nc.tensor.transpose(bank[:, :, h, u, :], raw_words[:, first : first + P], sorter[:])
                     view = words.rearrange("w (p g h c u) -> w p g h c u", p=PARITIES, g=CHUNK_PASSES, h=2, u=2)
-                    for parity in range(PARITIES):
-                        columns = slice(parity * P // 2, (parity + 1) * P // 2)
-                        copy_out(g, view[:, parity, g], bank[:, :, :, columns].rearrange("w h u c -> w h c u"))
+                    copy_out(bank_index, view[:, :, g], bank[:].rearrange("w p h u c -> w p h c u"))
                 else:
-                    view = words.rearrange("w (g l f u) -> w g l f u", g=CHUNK_PASSES, l=2, u=2)
-                    copy_out(g, view[:, g], bank[:].rearrange("w l u f -> w l f u"))
+                    g, pair = bank_index // 2, bank_index % 2
+                    bank = bank_pool.tile([P, 2, 2, P], F32, name="weight_bank", tag="bank")
+                    for l in range(2):
+                        raw_words = rnd["raw"][:, 2 * pair + l, :].bitcast(F32)
+                        for u in range(2):
+                            first = (2 * (2 * rnd["half"] + g) + u) * P
+                            nc.tensor.transpose(bank[:, l, u, :], raw_words[:, first : first + P], identity[:])
+                    view = words.rearrange("w (g l f u) -> w g l f u", g=2, l=DEGREES, u=2)
+                    copy_out(bank_index, view[:, g, 2 * pair : 2 * pair + 2], bank[:].rearrange("w l u f -> w l f u"))
             rnd["grouped"] = grouped
 
         def quantise(rnd):
             grouped = rnd["grouped"]
+            half_columns = ROUND_COLUMNS // 2
             if rnd["grads"]:
                 even_codes = even_pool.tile([P, CHUNK_PASSES * P], U32, name="even_codes", align_bytes=64)
                 even_scales = even_pool.tile([P, CHUNK_PASSES * P], U8, name="even_scales", align_bytes=64)
-                nc.vector.quantize_mx(out=even_codes[:].bitcast(E5M2_X4), scales=even_scales[:], in_=grouped[:, 0:CHUNK])
+                nc.vector.quantize_mx(
+                    out=even_codes[:].bitcast(E5M2_X4), scales=even_scales[:], in_=grouped[:, 0:half_columns]
+                )
                 kept = slice(rnd["chunk"] * CHUNK_PASSES * P, (rnd["chunk"] + 1) * CHUNK_PASSES * P)
                 nc.vector.quantize_mx(
                     out=odd_codes[:, rnd["r"], kept].bitcast(E5M2_X4),
                     scales=odd_scales[:, rnd["r"], kept],
-                    in_=grouped[:, CHUNK : 2 * CHUNK],
+                    in_=grouped[:, half_columns:ROUND_COLUMNS],
                 )
                 rnd["even"] = (even_codes, even_scales)
             else:
-                key = (rnd["parity"], rnd["chunk"])
-                if rnd["pair"] == 0:
-                    weight_codes = weight_pool.tile([P, CHUNK_PASSES, N_MOVING], U32, name="weight_codes", align_bytes=64)
-                    weight_scales = weight_pool.tile([P, CHUNK_PASSES, N_MOVING], U8, name="weight_scales", align_bytes=64)
-                    weights[key] = (weight_codes, weight_scales)
-                weight_codes, weight_scales = weights[key]
-                columns = slice(rnd["pair"] * 2 * F_IN, (rnd["pair"] + 1) * 2 * F_IN)
-                width = 2 * CHUNK // CHUNK_PASSES
-                for g in range(CHUNK_PASSES):
-                    nc.vector.quantize_mx(
-                        out=weight_codes[:, g, columns].bitcast(E4M3_X4),
-                        scales=weight_scales[:, g, columns],
-                        in_=grouped[:, g * width : (g + 1) * width],
-                    )
+                codes = weight_pool.tile([P, 2 * N_MOVING], U32, name="codes", align_bytes=64)
+                scales = weight_pool.tile([P, 2 * N_MOVING], U8, name="scales", align_bytes=64)
+                nc.vector.quantize_mx(out=codes[:].bitcast(E4M3_X4), scales=scales[:], in_=grouped[:])
+                for g in range(2):
+                    columns = slice(g * N_MOVING, (g + 1) * N_MOVING)
+                    whole_pass = rnd["chunk"] * CHUNK_PASSES + 2 * rnd["half"] + g
+                    weight_codes[(rnd["parity"], whole_pass)] = (codes[:, columns], scales[:, columns])
 
-        def passes(parity, r, chunk, grad_codes, grad_scales):
-            weight_codes, weight_scales = weights[(parity, chunk)]
-            if chunk == 0:
+        def one_pass(parity, r, whole_pass, grad_codes, grad_scales):
+            if whole_pass == 0:
                 sums[(parity, r)] = sum_pool.tile([P, N_MOVING], F32, name="sum%d" % r)
-            for g in range(CHUNK_PASSES):
-                rows = slice(g * P, (g + 1) * P)
-                nc.tensor.matmul_mx(
-                    out=sums[(parity, r)][:],
-                    lhsT=grad_codes[:, rows].bitcast(E5M2_X4),
-                    lhsT_scale=grad_scales[:, rows],
-                    rhs=weight_codes[:, g, :].bitcast(E4M3_X4),
-                    rhs_scale=weight_scales[:, g, :],
-                    start=(chunk == 0 and g == 0),
-                    stop=(chunk == CHUNKS - 1 and g == CHUNK_PASSES - 1),
-                )
+            codes, scales = weight_codes[(parity, whole_pass)]
+            nc.tensor.matmul_mx(
+                out=sums[(parity, r)][:],
+                lhsT=grad_codes.bitcast(E5M2_X4),
+                lhsT_scale=grad_scales,
+                rhs=codes.bitcast(E4M3_X4),
+                rhs_scale=scales,
+                start=(whole_pass == 0),
+                stop=(whole_pass == PASSES - 1),
+            )
+
+        def keep_own_degree(parity, r):
+            if r == 0:
+                results[parity] = result_pool.tile([P, ROW_TILES, F_IN], F32, name="result")
+            for quadrant in range(4):
+                rows = slice(quadrant * QUADRANT, (quadrant + 1) * QUADRANT)
+                degree = degree_of(8 * (quadrant % 2) + 4 * (quadrant // 2) + r)
+                own = sums[(parity, r)][rows, degree * F_IN : (degree + 1) * F_IN]
+                if quadrant % 2 == 0:
+                    nc.vector.tensor_copy(out=results[parity][rows, r, :], in_=own)
+                else:
+                    nc.scalar.copy(out=results[parity][rows, r, :], in_=own)
 
         def store(parity):
-            result = result_pool.tile([P, ROW_TILES, F_IN], F32, name="result")
-            for r in range(ROW_TILES):
-                for quadrant in range(4):
-                    rows = slice(quadrant * QUADRANT, (quadrant + 1) * QUADRANT)
-                    degree = degree_of(8 * (quadrant % 2) + 4 * (quadrant // 2) + r)
-                    kept = sums[(parity, r)][rows, degree * F_IN : (degree + 1) * F_IN]
-                    if quadrant % 2 == 0:
-                        nc.vector.tensor_copy(out=result[rows, r, :], in_=kept)
-                    else:
-                        nc.scalar.copy(out=result[rows, r, :], in_=kept)
             for quadrant in range(4):
                 rows = slice(quadrant * QUADRANT, (quadrant + 1) * QUADRANT)
                 first = 8 * (quadrant % 2) + 4 * (quadrant // 2)
                 nc.sync.dma_start(
                     out=out[:, parity, first : first + ROW_TILES, :].rearrange("n c f -> n (c f)"),
-                    in_=result[rows, :, :].rearrange("n r f -> n (r f)"),
+                    in_=results[parity][rows, :, :].rearrange("n r f -> n (r f)"),
                 )
 
         def multiply(rnd):
-            chunk = rnd["chunk"]
+            last_chunk = rnd["chunk"] == CHUNKS - 1
             if rnd["grads"]:
-                passes(0, rnd["r"], chunk, rnd["even"][0], rnd["even"][1])
-                if chunk == CHUNKS - 1 and rnd["r"] == ROW_TILES - 1:
-                    store(0)
-            elif rnd["parity"] == 1 and rnd["pair"] == 1:
-                kept = slice(chunk * CHUNK_PASSES * P, (chunk + 1) * CHUNK_PASSES * P)
+                r = rnd["r"]
+                for g in range(CHUNK_PASSES):
+                    rows = slice(g * P, (g + 1) * P)
+                    one_pass(EVEN, r, rnd["chunk"] * CHUNK_PASSES + g, rnd["even"][0][:, rows], rnd["even"][1][:, rows])
+                if last_chunk:
+                    keep_own_degree(EVEN, r)
+                    if r == ROW_TILES - 1:
+                        store(EVEN)
+            elif rnd["parity"] == ODD:
                 for r in range(ROW_TILES):
-                    passes(1, r, chunk, odd_codes[:, r, kept], odd_scales[:, r, kept])
-                if chunk == CHUNKS - 1:
-                    store(1)
+                    for g in range(2):
+                        whole_pass = rnd["chunk"] * CHUNK_PASSES + 2 * rnd["half"] + g
+                        rows = slice(whole_pass * P, (whole_pass + 1) * P)
+                        one_pass(ODD, r, whole_pass, odd_codes[:, r, rows], odd_scales[:, r, rows])
+                    if last_chunk and rnd["half"] == 1:
+                        keep_own_degree(ODD, r)
+                if last_chunk and rnd["half"] == 1:
+                    store(ODD)
 
-        for rnd in rounds[:RAW_BUFS]:
-            load(rnd)
         for step in range(len(rounds) + 2):
             if step < len(rounds):
                 transpose(rounds[step])
-            if step + RAW_BUFS < len(rounds):
-                load(rounds[step + RAW_BUFS])
             if 0 <= step - 1 < len(rounds):
                 quantise(rounds[step - 1])
             if step - 2 >= 0:

@@ -23,8 +23,11 @@ CHUNK_PASSES = CHUNK // K_PASS
 ROW_TILES = ITEMS * COMPONENTS // P
 N_MOVING = DEGREES * F_IN
 QUADRANT = 32
-ROUND_BANKS = 4
-ROUND_COLUMNS = 4 * ROUND_BANKS * 2 * P
+ROUND_COLUMNS = 2 * CHUNK
+
+BURST = {EVEN: 3, ODD: 8}
+
+RAW_BUFS = 13
 
 FLOPS = 2 * ITEMS * PARITIES * COMPONENTS * F_IN * F_OUT
 BYTES = 2 * (ITEMS * PARITIES * COMPONENTS + PARITIES * DEGREES * F_IN) * F_OUT + 4 * ITEMS * PARITIES * COMPONENTS * F_IN
@@ -38,18 +41,17 @@ def tile_dense_pa_k_kernel(tc, x, W_e, W_o, b, grad_out, out):
     nc = tc.nc
     with ExitStack() as ctx:
         const = ctx.enter_context(tc.tile_pool(name="const", bufs=1))
-        raw_weight_pool = ctx.enter_context(tc.tile_pool(name="raw_weights", bufs=3))
-        raw_grad_pool = ctx.enter_context(tc.tile_pool(name="raw_grads", bufs=8))
+        raw_pool = ctx.enter_context(tc.tile_pool(name="raw", bufs=RAW_BUFS))
         grouped_pool = ctx.enter_context(tc.tile_pool(name="grouped", bufs=3))
-        weight_pool = ctx.enter_context(tc.tile_pool(name="weight_codes", bufs=5))
-        even_pool = ctx.enter_context(tc.tile_pool(name="even_codes", bufs=3))
+        weight_pool = ctx.enter_context(tc.tile_pool(name="weight_codes", bufs=3))
+        even_pool = ctx.enter_context(tc.tile_pool(name="even_codes", bufs=4))
         result_pool = ctx.enter_context(tc.tile_pool(name="result", bufs=2))
-        bank_pool = ctx.enter_context(tc.psum_pool(name="banks", bufs=ROUND_BANKS))
+        bank_pool = ctx.enter_context(tc.psum_pool(name="banks", bufs=CHUNK_PASSES))
         sum_pool = ctx.enter_context(tc.psum_pool(name="sums", bufs=1))
         ctx.enter_context(tc.manual_schedule())
 
         grad_rows = grad_out.flatten_outer_dims().rearrange("(q h r) k -> r q h k", h=2, r=ROW_TILES)
-        weight_rows = [W.rearrange("l f k -> f l k") for W in (W_e, W_o)]
+        weight_rows = [W.rearrange("(a l) f k -> a f l k", l=2) for W in (W_e, W_o)]
 
         identity = const.tile([P, P], F32, name="identity")
         make_identity(nc, identity[:])
@@ -62,8 +64,8 @@ def tile_dense_pa_k_kernel(tc, x, W_e, W_o, b, grad_out, out):
         odd_codes = const.tile([P, ROW_TILES, PASSES * P], U32, name="odd_codes", align_bytes=64)
         odd_scales = const.tile([P, ROW_TILES, PASSES * P], U8, name="odd_scales", align_bytes=64)
 
-        def weight_round(parity, chunk, half):
-            return {"grads": False, "parity": parity, "chunk": chunk, "half": half}
+        def weight_round(parity, chunk, pair):
+            return {"grads": False, "parity": parity, "chunk": chunk, "pair": pair}
 
         rounds = [weight_round(EVEN, 0, 0), weight_round(EVEN, 0, 1)]
         for chunk in range(CHUNKS):
@@ -72,26 +74,22 @@ def tile_dense_pa_k_kernel(tc, x, W_e, W_o, b, grad_out, out):
                 if r % 2 == 0 and chunk + 1 < CHUNKS:
                     rounds.append(weight_round(EVEN, chunk + 1, r // 2))
         for chunk in range(CHUNKS):
-            for half in range(2):
-                rounds.append(weight_round(ODD, chunk, half))
+            for pair in range(2):
+                rounds.append(weight_round(ODD, chunk, pair))
 
-        raw_weights = {}
         for rnd in rounds:
             k_cols = slice(rnd["chunk"] * CHUNK, (rnd["chunk"] + 1) * CHUNK)
+            raw = raw_pool.tile([P, 2, CHUNK], BF16, name="raw")
             if rnd["grads"]:
-                raw_grads = raw_grad_pool.tile([P, 2, CHUNK], BF16, name="raw_grads")
-                nc.sync.dma_start(out=raw_grads[:], in_=grad_rows[rnd["r"]][:, :, k_cols])
-                rnd["raw"] = raw_grads
+                nc.sync.dma_start(out=raw[:], in_=grad_rows[rnd["r"]][:, :, k_cols])
             else:
-                if rnd["half"] == 0:
-                    raw_weight = raw_weight_pool.tile([P, DEGREES, CHUNK], BF16, name="raw_weight")
-                    nc.sync.dma_start(out=raw_weight[:], in_=weight_rows[rnd["parity"]][:, :, k_cols])
-                    raw_weights[(rnd["parity"], rnd["chunk"])] = raw_weight
-                rnd["raw"] = raw_weights[(rnd["parity"], rnd["chunk"])]
+                nc.sync.dma_start(out=raw[:], in_=weight_rows[rnd["parity"]][rnd["pair"]][:, :, k_cols])
+            rnd["raw"] = raw
 
-        weight_codes = {}
+        weights = {}
         sums = {}
         results = {}
+        ready = []
 
         def copy_out(bank_index, dst, src):
             if bank_index == 0:
@@ -102,115 +100,112 @@ def tile_dense_pa_k_kernel(tc, x, W_e, W_o, b, grad_out, out):
         def transpose(rnd):
             grouped = grouped_pool.tile([P, ROUND_COLUMNS], BF16, name="grouped", align_bytes=64)
             words = grouped[:].bitcast(F32)
-            for bank_index in range(ROUND_BANKS):
+            for g in range(CHUNK_PASSES):
                 if rnd["grads"]:
-                    g = bank_index
                     bank = bank_pool.tile([P, PARITIES, 2, 2, P // 2], F32, name="grad_bank", tag="bank")
-                    for h in range(2):
-                        raw_words = rnd["raw"][:, h, :].bitcast(F32)
-                        for u in range(2):
-                            first = (2 * g + u) * P
-                            nc.tensor.transpose(bank[:, :, h, u, :], raw_words[:, first : first + P], sorter[:])
-                    view = words.rearrange("w (p g h c u) -> w p g h c u", p=PARITIES, g=CHUNK_PASSES, h=2, u=2)
-                    copy_out(bank_index, view[:, :, g], bank[:].rearrange("w p h u c -> w p h c u"))
                 else:
-                    g, pair = bank_index // 2, bank_index % 2
                     bank = bank_pool.tile([P, 2, 2, P], F32, name="weight_bank", tag="bank")
-                    for l in range(2):
-                        raw_words = rnd["raw"][:, 2 * pair + l, :].bitcast(F32)
-                        for u in range(2):
-                            first = (2 * (2 * rnd["half"] + g) + u) * P
-                            nc.tensor.transpose(bank[:, l, u, :], raw_words[:, first : first + P], identity[:])
-                    view = words.rearrange("w (g l f u) -> w g l f u", g=2, l=DEGREES, u=2)
-                    copy_out(bank_index, view[:, g, 2 * pair : 2 * pair + 2], bank[:].rearrange("w l u f -> w l f u"))
+                for block in range(2):
+                    raw_words = rnd["raw"][:, block, :].bitcast(F32)
+                    for u in range(2):
+                        first = (2 * g + u) * P
+                        if rnd["grads"]:
+                            nc.tensor.transpose(bank[:, :, block, u, :], raw_words[:, first : first + P], sorter[:])
+                        else:
+                            nc.tensor.transpose(bank[:, block, u, :], raw_words[:, first : first + P], identity[:])
+                if rnd["grads"]:
+                    view = words.rearrange("w (p g h c u) -> w p g h c u", p=PARITIES, g=CHUNK_PASSES, h=2, u=2)
+                    copy_out(g, view[:, :, g], bank[:].rearrange("w p h u c -> w p h c u"))
+                else:
+                    view = words.rearrange("w (g l f u) -> w g l f u", g=CHUNK_PASSES, l=2, u=2)
+                    copy_out(g, view[:, g], bank[:].rearrange("w l u f -> w l f u"))
             rnd["grouped"] = grouped
 
         def quantise(rnd):
             grouped = rnd["grouped"]
-            half_columns = ROUND_COLUMNS // 2
+            chunk = rnd["chunk"]
+            first_pass = chunk * CHUNK_PASSES
             if rnd["grads"]:
+                r = rnd["r"]
                 even_codes = even_pool.tile([P, CHUNK_PASSES * P], U32, name="even_codes", align_bytes=64)
                 even_scales = even_pool.tile([P, CHUNK_PASSES * P], U8, name="even_scales", align_bytes=64)
+                nc.vector.quantize_mx(out=even_codes[:].bitcast(E5M2_X4), scales=even_scales[:], in_=grouped[:, 0:CHUNK])
+                kept = slice(first_pass * P, (first_pass + CHUNK_PASSES) * P)
                 nc.vector.quantize_mx(
-                    out=even_codes[:].bitcast(E5M2_X4), scales=even_scales[:], in_=grouped[:, 0:half_columns]
+                    out=odd_codes[:, r, kept].bitcast(E5M2_X4),
+                    scales=odd_scales[:, r, kept],
+                    in_=grouped[:, CHUNK:ROUND_COLUMNS],
                 )
-                kept = slice(rnd["chunk"] * CHUNK_PASSES * P, (rnd["chunk"] + 1) * CHUNK_PASSES * P)
-                nc.vector.quantize_mx(
-                    out=odd_codes[:, rnd["r"], kept].bitcast(E5M2_X4),
-                    scales=odd_scales[:, rnd["r"], kept],
-                    in_=grouped[:, half_columns:ROUND_COLUMNS],
-                )
-                rnd["even"] = (even_codes, even_scales)
+                for g in range(CHUNK_PASSES):
+                    rows = slice(g * P, (g + 1) * P)
+                    ready.append((EVEN, r, first_pass + g, even_codes[:, rows], even_scales[:, rows]))
             else:
-                codes = weight_pool.tile([P, 2 * N_MOVING], U32, name="codes", align_bytes=64)
-                scales = weight_pool.tile([P, 2 * N_MOVING], U8, name="scales", align_bytes=64)
-                nc.vector.quantize_mx(out=codes[:].bitcast(E4M3_X4), scales=scales[:], in_=grouped[:])
-                for g in range(2):
-                    columns = slice(g * N_MOVING, (g + 1) * N_MOVING)
-                    whole_pass = rnd["chunk"] * CHUNK_PASSES + 2 * rnd["half"] + g
-                    weight_codes[(rnd["parity"], whole_pass)] = (codes[:, columns], scales[:, columns])
+                key = (rnd["parity"], chunk)
+                if rnd["pair"] == 0:
+                    weight_codes = weight_pool.tile([P, CHUNK_PASSES, N_MOVING], U32, name="weight_codes", align_bytes=64)
+                    weight_scales = weight_pool.tile([P, CHUNK_PASSES, N_MOVING], U8, name="weight_scales", align_bytes=64)
+                    weights[key] = (weight_codes, weight_scales)
+                weight_codes, weight_scales = weights[key]
+                columns = slice(rnd["pair"] * 2 * F_IN, (rnd["pair"] + 1) * 2 * F_IN)
+                width = ROUND_COLUMNS // CHUNK_PASSES
+                for g in range(CHUNK_PASSES):
+                    nc.vector.quantize_mx(
+                        out=weight_codes[:, g, columns].bitcast(E4M3_X4),
+                        scales=weight_scales[:, g, columns],
+                        in_=grouped[:, g * width : (g + 1) * width],
+                    )
+                if rnd["parity"] == ODD and rnd["pair"] == 1:
+                    for r in range(ROW_TILES):
+                        for g in range(first_pass, first_pass + CHUNK_PASSES):
+                            rows = slice(g * P, (g + 1) * P)
+                            ready.append((ODD, r, g, odd_codes[:, r, rows], odd_scales[:, r, rows]))
 
         def one_pass(parity, r, whole_pass, grad_codes, grad_scales):
             if whole_pass == 0:
                 sums[(parity, r)] = sum_pool.tile([P, N_MOVING], F32, name="sum%d" % r)
-            codes, scales = weight_codes[(parity, whole_pass)]
+            weight_codes, weight_scales = weights[(parity, whole_pass // CHUNK_PASSES)]
+            g = whole_pass % CHUNK_PASSES
             nc.tensor.matmul_mx(
                 out=sums[(parity, r)][:],
                 lhsT=grad_codes.bitcast(E5M2_X4),
                 lhsT_scale=grad_scales,
-                rhs=codes.bitcast(E4M3_X4),
-                rhs_scale=scales,
+                rhs=weight_codes[:, g, :].bitcast(E4M3_X4),
+                rhs_scale=weight_scales[:, g, :],
                 start=(whole_pass == 0),
                 stop=(whole_pass == PASSES - 1),
             )
 
-        def keep_own_degree(parity, r):
+        def finish(parity, r):
             if r == 0:
                 results[parity] = result_pool.tile([P, ROW_TILES, F_IN], F32, name="result")
             for quadrant in range(4):
                 rows = slice(quadrant * QUADRANT, (quadrant + 1) * QUADRANT)
-                degree = degree_of(8 * (quadrant % 2) + 4 * (quadrant // 2) + r)
+                first = 8 * (quadrant % 2) + 4 * (quadrant // 2)
+                degree = degree_of(first + r)
                 own = sums[(parity, r)][rows, degree * F_IN : (degree + 1) * F_IN]
                 if quadrant % 2 == 0:
                     nc.vector.tensor_copy(out=results[parity][rows, r, :], in_=own)
                 else:
                     nc.scalar.copy(out=results[parity][rows, r, :], in_=own)
+                if r == ROW_TILES - 1:
+                    nc.sync.dma_start(
+                        out=out[:, parity, first : first + ROW_TILES, :].rearrange("n c f -> n (c f)"),
+                        in_=results[parity][rows, :, :].rearrange("n r f -> n (r f)"),
+                    )
 
-        def store(parity):
-            for quadrant in range(4):
-                rows = slice(quadrant * QUADRANT, (quadrant + 1) * QUADRANT)
-                first = 8 * (quadrant % 2) + 4 * (quadrant // 2)
-                nc.sync.dma_start(
-                    out=out[:, parity, first : first + ROW_TILES, :].rearrange("n c f -> n (c f)"),
-                    in_=results[parity][rows, :, :].rearrange("n r f -> n (r f)"),
-                )
-
-        def multiply(rnd):
-            last_chunk = rnd["chunk"] == CHUNKS - 1
-            if rnd["grads"]:
-                r = rnd["r"]
-                for g in range(CHUNK_PASSES):
-                    rows = slice(g * P, (g + 1) * P)
-                    one_pass(EVEN, r, rnd["chunk"] * CHUNK_PASSES + g, rnd["even"][0][:, rows], rnd["even"][1][:, rows])
-                if last_chunk:
-                    keep_own_degree(EVEN, r)
-                    if r == ROW_TILES - 1:
-                        store(EVEN)
-            elif rnd["parity"] == ODD:
-                for r in range(ROW_TILES):
-                    for g in range(2):
-                        whole_pass = rnd["chunk"] * CHUNK_PASSES + 2 * rnd["half"] + g
-                        rows = slice(whole_pass * P, (whole_pass + 1) * P)
-                        one_pass(ODD, r, whole_pass, odd_codes[:, r, rows], odd_scales[:, r, rows])
-                    if last_chunk and rnd["half"] == 1:
-                        keep_own_degree(ODD, r)
-                if last_chunk and rnd["half"] == 1:
-                    store(ODD)
-
-        for step in range(len(rounds) + 2):
+        for step in range(len(rounds) + 1):
             if step < len(rounds):
                 transpose(rounds[step])
-            if 0 <= step - 1 < len(rounds):
+            burst = ready[: BURST[ready[0][0]]] if ready else []
+            ready = ready[len(burst) :]
+            for job in burst:
+                one_pass(*job)
+            if step >= 1:
                 quantise(rounds[step - 1])
-            if step - 2 >= 0:
-                multiply(rounds[step - 2])
+            for job in burst:
+                if job[2] == PASSES - 1:
+                    finish(job[0], job[1])
+        for job in ready:
+            one_pass(*job)
+            if job[2] == PASSES - 1:
+                finish(job[0], job[1])

@@ -11,30 +11,37 @@ E4M3_X4 = mybir.dt.float8_e4m3fn_x4
 E5M2_X4 = mybir.dt.float8_e5m2_x4
 
 ITEMS, PARITIES, COMPONENTS, DEGREES = 32, 2, 16, 4
-EVEN, ODD = 0, 1
 F_IN, F_OUT = 128, 8192
 
 P = 128
 K_PASS = 4 * P
 PASSES = F_OUT // K_PASS
-CHUNK = 2048
-CHUNKS = F_OUT // CHUNK
-CHUNK_PASSES = CHUNK // K_PASS
-ROW_TILES = ITEMS * COMPONENTS // P
-N_MOVING = DEGREES * F_IN
+MAX_CHUNK = 4
+HALF_TILES = 4
+N_MOVING = 4 * F_IN
 QUADRANT = 32
-ROUND_COLUMNS = 2 * CHUNK
+PASS_WORDS = 2 * P
 
-BURST = {EVEN: 3, ODD: 8}
+HALVES = ((1, (1, 1, 2, 4, 4, 4)), (0, (4, 4, 4, 4)))
 
-RAW_BUFS = 13
+RUN = 4
+BURST = 4
+
+RAW_BUFS = 8
+CODE_BUFS = 4
 
 FLOPS = 2 * ITEMS * PARITIES * COMPONENTS * F_IN * F_OUT
 BYTES = 2 * (ITEMS * PARITIES * COMPONENTS + PARITIES * DEGREES * F_IN) * F_OUT + 4 * ITEMS * PARITIES * COMPONENTS * F_IN
 
 
-def degree_of(component):
-    return sum(1 for l in range(1, DEGREES) if component >= l * l)
+def window_of(j):
+    if j == 0:
+        return 0
+    return N_MOVING if j < HALF_TILES else N_MOVING // 2
+
+
+def own_block(j, quadrant):
+    return (quadrant + 2) % 4 if 0 < j < HALF_TILES else quadrant
 
 
 def tile_dense_pa_k_kernel(tc, x, W_e, W_o, b, grad_out, out):
@@ -42,170 +49,173 @@ def tile_dense_pa_k_kernel(tc, x, W_e, W_o, b, grad_out, out):
     with ExitStack() as ctx:
         const = ctx.enter_context(tc.tile_pool(name="const", bufs=1))
         raw_pool = ctx.enter_context(tc.tile_pool(name="raw", bufs=RAW_BUFS))
-        grouped_pool = ctx.enter_context(tc.tile_pool(name="grouped", bufs=3))
-        weight_pool = ctx.enter_context(tc.tile_pool(name="weight_codes", bufs=3))
-        even_pool = ctx.enter_context(tc.tile_pool(name="even_codes", bufs=4))
+        grouped_w_pool = ctx.enter_context(tc.tile_pool(name="grouped_w", bufs=2))
+        grouped_g_pool = ctx.enter_context(tc.tile_pool(name="grouped_g", bufs=3))
+        code_pool = ctx.enter_context(tc.tile_pool(name="grad_codes", bufs=CODE_BUFS))
         result_pool = ctx.enter_context(tc.tile_pool(name="result", bufs=2))
-        bank_pool = ctx.enter_context(tc.psum_pool(name="banks", bufs=CHUNK_PASSES))
+        bank_pool = ctx.enter_context(tc.psum_pool(name="banks", bufs=4))
         sum_pool = ctx.enter_context(tc.psum_pool(name="sums", bufs=1))
         ctx.enter_context(tc.manual_schedule())
 
-        grad_rows = grad_out.flatten_outer_dims().rearrange("(q h r) k -> r q h k", h=2, r=ROW_TILES)
-        weight_rows = [W.rearrange("(a l) f k -> a f l k", l=2) for W in (W_e, W_o)]
+        grad_rows = grad_out.flatten_outer_dims().rearrange("(q h v s) k -> h v q s k", h=2, v=2, s=2)
+        weight_rows = [W.rearrange("(h l) f k -> h f l k", l=2) for W in (W_e, W_o)]
 
         identity = const.tile([P, P], F32, name="identity")
         make_identity(nc, identity[:])
         sorter = const.tile([P, P], F32, name="sorter")
         nc.vector.tensor_copy(
-            out=sorter[:].rearrange("i (p x n) -> i p x n", p=PARITIES, x=2),
-            in_=identity[:].rearrange("i (n p x) -> i p x n", p=PARITIES, x=2),
+            out=sorter[:].rearrange("i (x p n) -> i x p n", p=PARITIES, x=2),
+            in_=identity[:].rearrange("i (n p x) -> i x p n", p=PARITIES, x=2),
         )
 
-        odd_codes = const.tile([P, ROW_TILES, PASSES * P], U32, name="odd_codes", align_bytes=64)
-        odd_scales = const.tile([P, ROW_TILES, PASSES * P], U8, name="odd_scales", align_bytes=64)
+        weight_codes = const.tile([P, PASSES, 2 * N_MOVING], U32, name="weight_codes", align_bytes=64)
+        weight_scales = const.tile([P, PASSES, 2 * N_MOVING], U8, name="weight_scales", align_bytes=64)
 
-        def weight_round(parity, chunk, pair):
-            return {"grads": False, "parity": parity, "chunk": chunk, "pair": pair}
+        chunks = []
+        for h, sizes in HALVES:
+            first = 0
+            for size in sizes:
+                chunks.append({"h": h, "first": first, "size": size})
+                first += size
+            assert first == PASSES
 
-        rounds = [weight_round(EVEN, 0, 0), weight_round(EVEN, 0, 1)]
-        for chunk in range(CHUNKS):
-            for r in range(ROW_TILES):
-                rounds.append({"grads": True, "chunk": chunk, "r": r})
-                if r % 2 == 0 and chunk + 1 < CHUNKS:
-                    rounds.append(weight_round(EVEN, chunk + 1, r // 2))
-        for chunk in range(CHUNKS):
-            for pair in range(2):
-                rounds.append(weight_round(ODD, chunk, pair))
+        def weight_round(chunk, parity):
+            return {"grads": False, "chunk": chunk, "parity": parity}
+
+        rounds = [weight_round(chunks[0], 0), weight_round(chunks[0], 1)]
+        for i, chunk in enumerate(chunks):
+            for v in range(2):
+                rounds.append({"grads": True, "chunk": chunk, "v": v})
+                if i + 1 < len(chunks):
+                    rounds.append(weight_round(chunks[i + 1], v))
 
         for rnd in rounds:
-            k_cols = slice(rnd["chunk"] * CHUNK, (rnd["chunk"] + 1) * CHUNK)
-            raw = raw_pool.tile([P, 2, CHUNK], BF16, name="raw")
+            chunk = rnd["chunk"]
+            width = chunk["size"] * K_PASS
+            k_cols = slice(chunk["first"] * K_PASS, chunk["first"] * K_PASS + width)
+            raw = raw_pool.tile([P, 2, MAX_CHUNK * K_PASS], BF16, name="raw")
             if rnd["grads"]:
-                nc.sync.dma_start(out=raw[:], in_=grad_rows[rnd["r"]][:, :, k_cols])
+                nc.sync.dma_start(out=raw[:, :, 0:width], in_=grad_rows[chunk["h"]][rnd["v"]][:, :, k_cols])
             else:
-                nc.sync.dma_start(out=raw[:], in_=weight_rows[rnd["parity"]][rnd["pair"]][:, :, k_cols])
+                nc.sync.dma_start(out=raw[:, :, 0:width], in_=weight_rows[rnd["parity"]][chunk["h"]][:, :, k_cols])
             rnd["raw"] = raw
 
-        weights = {}
         sums = {}
         results = {}
         ready = []
+        counters = {"unit": 0}
 
-        def copy_out(bank_index, dst, src):
-            if bank_index == 0:
+        def unit(rnd, g):
+            chunk = rnd["chunk"]
+            if g == 0:
+                if rnd["grads"]:
+                    rnd["grouped"] = grouped_g_pool.tile([P, MAX_CHUNK * 2 * K_PASS], BF16, name="grouped_g", align_bytes=64)
+                elif rnd["parity"] == 0:
+                    chunk["grouped"] = grouped_w_pool.tile([P, MAX_CHUNK * 4 * K_PASS], BF16, name="grouped_w", align_bytes=64)
+            bank = bank_pool.tile([P, 2, 2, P], F32, name="bank")
+            for block in range(2):
+                raw_words = rnd["raw"][:, block, :].bitcast(F32)
+                for u in range(2):
+                    first = (2 * g + u) * P
+                    nc.tensor.transpose(bank[:, block, u, :], raw_words[:, first : first + P], sorter[:] if rnd["grads"] else identity[:])
+            if rnd["grads"]:
+                words = rnd["grouped"][:].bitcast(F32).rearrange("w (g s c u) -> w g s c u", g=MAX_CHUNK, s=2, u=2)
+                dst = words[:, g]
+            else:
+                words = chunk["grouped"][:].bitcast(F32).rearrange("w (g l p f u) -> w g l p f u", g=MAX_CHUNK, l=2, p=PARITIES, u=2)
+                dst = words[:, g, :, rnd["parity"]]
+            src = bank[:].rearrange("w s u c -> w s c u")
+            if counters["unit"] % 4 == 0:
                 nc.vector.tensor_copy(out=dst, in_=src)
             else:
                 nc.scalar.copy(out=dst, in_=src)
-
-        def transpose(rnd):
-            grouped = grouped_pool.tile([P, ROUND_COLUMNS], BF16, name="grouped", align_bytes=64)
-            words = grouped[:].bitcast(F32)
-            for g in range(CHUNK_PASSES):
-                if rnd["grads"]:
-                    bank = bank_pool.tile([P, PARITIES, 2, 2, P // 2], F32, name="grad_bank", tag="bank")
-                else:
-                    bank = bank_pool.tile([P, 2, 2, P], F32, name="weight_bank", tag="bank")
-                for block in range(2):
-                    raw_words = rnd["raw"][:, block, :].bitcast(F32)
-                    for u in range(2):
-                        first = (2 * g + u) * P
-                        if rnd["grads"]:
-                            nc.tensor.transpose(bank[:, :, block, u, :], raw_words[:, first : first + P], sorter[:])
-                        else:
-                            nc.tensor.transpose(bank[:, block, u, :], raw_words[:, first : first + P], identity[:])
-                if rnd["grads"]:
-                    view = words.rearrange("w (p g h c u) -> w p g h c u", p=PARITIES, g=CHUNK_PASSES, h=2, u=2)
-                    copy_out(g, view[:, :, g], bank[:].rearrange("w p h u c -> w p h c u"))
-                else:
-                    view = words.rearrange("w (g l f u) -> w g l f u", g=CHUNK_PASSES, l=2, u=2)
-                    copy_out(g, view[:, g], bank[:].rearrange("w l u f -> w l f u"))
-            rnd["grouped"] = grouped
+            counters["unit"] += 1
 
         def quantise(rnd):
-            grouped = rnd["grouped"]
             chunk = rnd["chunk"]
-            first_pass = chunk * CHUNK_PASSES
+            size = chunk["size"]
             if rnd["grads"]:
-                r = rnd["r"]
-                even_codes = even_pool.tile([P, CHUNK_PASSES * P], U32, name="even_codes", align_bytes=64)
-                even_scales = even_pool.tile([P, CHUNK_PASSES * P], U8, name="even_scales", align_bytes=64)
-                nc.vector.quantize_mx(out=even_codes[:].bitcast(E5M2_X4), scales=even_scales[:], in_=grouped[:, 0:CHUNK])
-                kept = slice(first_pass * P, (first_pass + CHUNK_PASSES) * P)
+                assert len(ready) <= (CODE_BUFS - 1) * 2 * MAX_CHUNK
+                codes = code_pool.tile([P, MAX_CHUNK * 2 * P], U32, name="grad_codes", align_bytes=64)
+                scales = code_pool.tile([P, MAX_CHUNK * 2 * P], U8, name="grad_scales", align_bytes=64)
                 nc.vector.quantize_mx(
-                    out=odd_codes[:, r, kept].bitcast(E5M2_X4),
-                    scales=odd_scales[:, r, kept],
-                    in_=grouped[:, CHUNK:ROUND_COLUMNS],
+                    out=codes[:, 0 : size * 2 * P].bitcast(E5M2_X4),
+                    scales=scales[:, 0 : size * 2 * P],
+                    in_=rnd["grouped"][:, 0 : size * 2 * K_PASS],
                 )
-                for g in range(CHUNK_PASSES):
-                    rows = slice(g * P, (g + 1) * P)
-                    ready.append((EVEN, r, first_pass + g, even_codes[:, rows], even_scales[:, rows]))
-            else:
-                key = (rnd["parity"], chunk)
-                if rnd["pair"] == 0:
-                    weight_codes = weight_pool.tile([P, CHUNK_PASSES, N_MOVING], U32, name="weight_codes", align_bytes=64)
-                    weight_scales = weight_pool.tile([P, CHUNK_PASSES, N_MOVING], U8, name="weight_scales", align_bytes=64)
-                    weights[key] = (weight_codes, weight_scales)
-                weight_codes, weight_scales = weights[key]
-                columns = slice(rnd["pair"] * 2 * F_IN, (rnd["pair"] + 1) * 2 * F_IN)
-                width = ROUND_COLUMNS // CHUNK_PASSES
-                for g in range(CHUNK_PASSES):
-                    nc.vector.quantize_mx(
-                        out=weight_codes[:, g, columns].bitcast(E4M3_X4),
-                        scales=weight_scales[:, g, columns],
-                        in_=grouped[:, g * width : (g + 1) * width],
-                    )
-                if rnd["parity"] == ODD and rnd["pair"] == 1:
-                    for r in range(ROW_TILES):
-                        for g in range(first_pass, first_pass + CHUNK_PASSES):
-                            rows = slice(g * P, (g + 1) * P)
-                            ready.append((ODD, r, g, odd_codes[:, r, rows], odd_scales[:, r, rows]))
+                for s in range(2):
+                    for g in range(size):
+                        rows = slice((2 * g + s) * P, (2 * g + s + 1) * P)
+                        ready.append((4 * chunk["h"] + 2 * rnd["v"] + s, chunk["first"] + g, codes[:, rows], scales[:, rows]))
+            elif rnd["parity"] == 1:
+                grouped = chunk["grouped"]
+                for g in range(size):
+                    whole_pass = chunk["first"] + g
+                    if chunk["h"] == 1:
+                        pieces = [(g * 4 * K_PASS, 4 * K_PASS, N_MOVING // 2)]
+                    else:
+                        pieces = [(g * 4 * K_PASS, 2 * K_PASS, 0), (g * 4 * K_PASS + 2 * K_PASS, 2 * K_PASS, 3 * N_MOVING // 2)]
+                    for start, width, column in pieces:
+                        nc.vector.quantize_mx(
+                            out=weight_codes[:, whole_pass, column : column + width // 4].bitcast(E4M3_X4),
+                            scales=weight_scales[:, whole_pass, column : column + width // 4],
+                            in_=grouped[:, start : start + width],
+                        )
 
-        def one_pass(parity, r, whole_pass, grad_codes, grad_scales):
+        def one_pass(j, whole_pass, grad_codes, grad_scales):
             if whole_pass == 0:
-                sums[(parity, r)] = sum_pool.tile([P, N_MOVING], F32, name="sum%d" % r)
-            weight_codes, weight_scales = weights[(parity, whole_pass // CHUNK_PASSES)]
-            g = whole_pass % CHUNK_PASSES
+                sums[j] = sum_pool.tile([P, N_MOVING], F32, name="sum%d" % (j % HALF_TILES))
+            columns = slice(window_of(j), window_of(j) + N_MOVING)
             nc.tensor.matmul_mx(
-                out=sums[(parity, r)][:],
+                out=sums[j][:],
                 lhsT=grad_codes.bitcast(E5M2_X4),
                 lhsT_scale=grad_scales,
-                rhs=weight_codes[:, g, :].bitcast(E4M3_X4),
-                rhs_scale=weight_scales[:, g, :],
+                rhs=weight_codes[:, whole_pass, columns].bitcast(E4M3_X4),
+                rhs_scale=weight_scales[:, whole_pass, columns],
                 start=(whole_pass == 0),
                 stop=(whole_pass == PASSES - 1),
             )
 
-        def finish(parity, r):
+        def finish(j):
+            h, r = j // HALF_TILES, j % HALF_TILES
             if r == 0:
-                results[parity] = result_pool.tile([P, ROW_TILES, F_IN], F32, name="result")
+                results[h] = result_pool.tile([P, HALF_TILES, F_IN], F32, name="result")
             for quadrant in range(4):
                 rows = slice(quadrant * QUADRANT, (quadrant + 1) * QUADRANT)
-                first = 8 * (quadrant % 2) + 4 * (quadrant // 2)
-                degree = degree_of(first + r)
-                own = sums[(parity, r)][rows, degree * F_IN : (degree + 1) * F_IN]
+                block = own_block(j, quadrant)
+                own = sums[j][rows, block * F_IN : (block + 1) * F_IN]
                 if quadrant % 2 == 0:
-                    nc.vector.tensor_copy(out=results[parity][rows, r, :], in_=own)
+                    nc.vector.tensor_copy(out=results[h][rows, r, :], in_=own)
                 else:
-                    nc.scalar.copy(out=results[parity][rows, r, :], in_=own)
-                if r == ROW_TILES - 1:
+                    nc.scalar.copy(out=results[h][rows, r, :], in_=own)
+                if r == HALF_TILES - 1:
+                    first = 8 * (quadrant // 2) + HALF_TILES * h
                     nc.sync.dma_start(
-                        out=out[:, parity, first : first + ROW_TILES, :].rearrange("n c f -> n (c f)"),
-                        in_=results[parity][rows, :, :].rearrange("n r f -> n (r f)"),
+                        out=out[:, quadrant % 2, first : first + HALF_TILES, :].rearrange("n c f -> n (c f)"),
+                        in_=results[h][rows, :, :].rearrange("n r f -> n (r f)"),
                     )
 
-        for step in range(len(rounds) + 1):
-            if step < len(rounds):
-                transpose(rounds[step])
-            burst = ready[: BURST[ready[0][0]]] if ready else []
+        units = [(rnd, g) for rnd in rounds for g in range(rnd["chunk"]["size"])]
+        copied = []
+        for position in range(0, len(units), RUN):
+            completed = []
+            for rnd, g in units[position : position + RUN]:
+                unit(rnd, g)
+                if g == rnd["chunk"]["size"] - 1:
+                    completed.append(rnd)
+            burst = ready[:BURST]
             ready = ready[len(burst) :]
             for job in burst:
                 one_pass(*job)
-            if step >= 1:
-                quantise(rounds[step - 1])
+            for rnd in copied:
+                quantise(rnd)
+            copied = completed
             for job in burst:
-                if job[2] == PASSES - 1:
-                    finish(job[0], job[1])
+                if job[1] == PASSES - 1:
+                    finish(job[0])
+        for rnd in copied:
+            quantise(rnd)
         for job in ready:
             one_pass(*job)
-            if job[2] == PASSES - 1:
-                finish(job[0], job[1])
+            if job[1] == PASSES - 1:
+                finish(job[0])

@@ -24,8 +24,13 @@ PASS_WORDS = 2 * P
 
 HALVES = ((1, (1, 1, 2, 4, 4, 4)), (0, (4, 4, 4, 4)))
 
-RUN = 4
-BURST = 4
+HEAD_RUN = 4
+HEAD_UNITS = 16
+RUN = 6
+BURST = 6
+LAG = 2
+PASS_LAG = 3
+COPY_MOD = 4
 
 RAW_BUFS = 8
 CODE_BUFS = 4
@@ -104,6 +109,7 @@ def tile_dense_pa_k_kernel(tc, x, W_e, W_o, b, grad_out, out):
         results = {}
         ready = []
         counters = {"unit": 0}
+        pieces = []
 
         def unit(rnd, g):
             chunk = rnd["chunk"]
@@ -125,44 +131,50 @@ def tile_dense_pa_k_kernel(tc, x, W_e, W_o, b, grad_out, out):
                 words = chunk["grouped"][:].bitcast(F32).rearrange("w (g l p f u) -> w g l p f u", g=MAX_CHUNK, l=2, p=PARITIES, u=2)
                 dst = words[:, g, :, rnd["parity"]]
             src = bank[:].rearrange("w s u c -> w s c u")
-            if counters["unit"] % 4 == 0:
+            if counters["unit"] % COPY_MOD == 0:
                 nc.vector.tensor_copy(out=dst, in_=src)
             else:
                 nc.scalar.copy(out=dst, in_=src)
             counters["unit"] += 1
-
-        def quantise(rnd):
-            chunk = rnd["chunk"]
             size = chunk["size"]
             if rnd["grads"]:
-                assert len(ready) <= (CODE_BUFS - 1) * 2 * MAX_CHUNK
-                codes = code_pool.tile([P, MAX_CHUNK * 2 * P], U32, name="grad_codes", align_bytes=64)
-                scales = code_pool.tile([P, MAX_CHUNK * 2 * P], U8, name="grad_scales", align_bytes=64)
-                nc.vector.quantize_mx(
-                    out=codes[:, 0 : size * 2 * P].bitcast(E5M2_X4),
-                    scales=scales[:, 0 : size * 2 * P],
-                    in_=rnd["grouped"][:, 0 : size * 2 * K_PASS],
-                )
-                for s in range(2):
-                    for g in range(size):
-                        rows = slice((2 * g + s) * P, (2 * g + s + 1) * P)
-                        ready.append((4 * chunk["h"] + 2 * rnd["v"] + s, chunk["first"] + g, codes[:, rows], scales[:, rows]))
+                if g % 2 == 1 or g == size - 1:
+                    pieces.append((counters["unit"], rnd, g - g % 2, g + 1))
             elif rnd["parity"] == 1:
+                pieces.append((counters["unit"], rnd, g, g + 1))
+
+        def quantise(rnd, g0, g1):
+            chunk = rnd["chunk"]
+            if rnd["grads"]:
+                if g0 == 0:
+                    rnd["codes"] = code_pool.tile([P, MAX_CHUNK * 2 * P], U32, name="grad_codes", align_bytes=64)
+                    rnd["scales"] = code_pool.tile([P, MAX_CHUNK * 2 * P], U8, name="grad_scales", align_bytes=64)
+                codes, scales = rnd["codes"], rnd["scales"]
+                nc.vector.quantize_mx(
+                    out=codes[:, g0 * 2 * P : g1 * 2 * P].bitcast(E5M2_X4),
+                    scales=scales[:, g0 * 2 * P : g1 * 2 * P],
+                    in_=rnd["grouped"][:, g0 * 2 * K_PASS : g1 * 2 * K_PASS],
+                )
+                for g in range(g0, g1):
+                    for s in range(2):
+                        rows = slice((2 * g + s) * P, (2 * g + s + 1) * P)
+                        ready.append((4 * chunk["h"] + 2 * rnd["v"] + s, chunk["first"] + g, codes[:, rows], scales[:, rows], counters["unit"]))
+            else:
                 grouped = chunk["grouped"]
-                for g in range(size):
+                for g in range(g0, g1):
                     whole_pass = chunk["first"] + g
                     if chunk["h"] == 1:
-                        pieces = [(g * 4 * K_PASS, 4 * K_PASS, N_MOVING // 2)]
+                        parts = [(g * 4 * K_PASS, 4 * K_PASS, N_MOVING // 2)]
                     else:
-                        pieces = [(g * 4 * K_PASS, 2 * K_PASS, 0), (g * 4 * K_PASS + 2 * K_PASS, 2 * K_PASS, 3 * N_MOVING // 2)]
-                    for start, width, column in pieces:
+                        parts = [(g * 4 * K_PASS, 2 * K_PASS, 0), (g * 4 * K_PASS + 2 * K_PASS, 2 * K_PASS, 3 * N_MOVING // 2)]
+                    for start, width, column in parts:
                         nc.vector.quantize_mx(
                             out=weight_codes[:, whole_pass, column : column + width // 4].bitcast(E4M3_X4),
                             scales=weight_scales[:, whole_pass, column : column + width // 4],
                             in_=grouped[:, start : start + width],
                         )
 
-        def one_pass(j, whole_pass, grad_codes, grad_scales):
+        def one_pass(j, whole_pass, grad_codes, grad_scales, written):
             if whole_pass == 0:
                 sums[j] = sum_pool.tile([P, N_MOVING], F32, name="sum%d" % (j % HALF_TILES))
             columns = slice(window_of(j), window_of(j) + N_MOVING)
@@ -196,25 +208,23 @@ def tile_dense_pa_k_kernel(tc, x, W_e, W_o, b, grad_out, out):
                     )
 
         units = [(rnd, g) for rnd in rounds for g in range(rnd["chunk"]["size"])]
-        copied = []
-        for position in range(0, len(units), RUN):
-            completed = []
-            for rnd, g in units[position : position + RUN]:
+        position = 0
+        while position < len(units):
+            length = HEAD_RUN if position < HEAD_UNITS else RUN
+            for rnd, g in units[position : position + length]:
                 unit(rnd, g)
-                if g == rnd["chunk"]["size"] - 1:
-                    completed.append(rnd)
-            burst = ready[:BURST]
+                while pieces and pieces[0][0] + LAG <= counters["unit"]:
+                    quantise(*pieces.pop(0)[1:])
+            position += length
+            burst = [job for job in ready[: (HEAD_RUN if position <= HEAD_UNITS else BURST)] if job[4] + PASS_LAG <= counters["unit"]]
             ready = ready[len(burst) :]
             for job in burst:
                 one_pass(*job)
-            for rnd in copied:
-                quantise(rnd)
-            copied = completed
             for job in burst:
                 if job[1] == PASSES - 1:
                     finish(job[0])
-        for rnd in copied:
-            quantise(rnd)
+        while pieces:
+            quantise(*pieces.pop(0)[1:])
         for job in ready:
             one_pass(*job)
             if job[1] == PASSES - 1:

@@ -26,8 +26,8 @@ HALVES = ((1, (1, 1, 2, 4, 4, 4)), (0, (4, 4, 4, 4)))
 
 HEAD_RUN = 4
 HEAD_UNITS = 16
-RUN = 6
-BURST = 6
+RUN = 4
+BURST = 4
 LAG = 2
 PASS_LAG = 3
 COPY_MOD = 4

@@ -26,8 +26,8 @@ HALVES = ((1, (1, 1, 2, 4, 4, 4)), (0, (4, 4, 4, 4)))
 
 HEAD_RUN = 4
 HEAD_UNITS = 16
-RUN = 4
-BURST = 4
+RUN = 3
+BURST = 3
 LAG = 2
 PASS_LAG = 3
 COPY_MOD = 4

@@ -57,7 +57,7 @@ def tile_dense_pa_k_kernel(tc, x, W_e, W_o, b, grad_out, out):
         grouped_w_pool = ctx.enter_context(tc.tile_pool(name="grouped_w", bufs=2))
         grouped_g_pool = ctx.enter_context(tc.tile_pool(name="grouped_g", bufs=3))
         code_pool = ctx.enter_context(tc.tile_pool(name="grad_codes", bufs=CODE_BUFS))
-        result_pool = ctx.enter_context(tc.tile_pool(name="result", bufs=2))
+        result_pool = ctx.enter_context(tc.tile_pool(name="result", bufs=HALF_TILES))
         bank_pool = ctx.enter_context(tc.psum_pool(name="banks", bufs=4))
         sum_pool = ctx.enter_context(tc.psum_pool(name="sums", bufs=1))
         ctx.enter_context(tc.manual_schedule())
@@ -106,7 +106,6 @@ def tile_dense_pa_k_kernel(tc, x, W_e, W_o, b, grad_out, out):
             rnd["raw"] = raw
 
         sums = {}
-        results = {}
         ready = []
         counters = {"unit": 0}
         pieces = []
@@ -189,23 +188,18 @@ def tile_dense_pa_k_kernel(tc, x, W_e, W_o, b, grad_out, out):
             )
 
         def finish(j):
-            h, r = j // HALF_TILES, j % HALF_TILES
-            if r == 0:
-                results[h] = result_pool.tile([P, HALF_TILES, F_IN], F32, name="result")
+            whole = result_pool.tile([P, N_MOVING], F32, name="whole")
+            if j % 2 == 0:
+                nc.scalar.copy(out=whole[:], in_=sums[j][:])
+            else:
+                nc.vector.tensor_copy(out=whole[:], in_=sums[j][:])
             for quadrant in range(4):
                 rows = slice(quadrant * QUADRANT, (quadrant + 1) * QUADRANT)
                 block = own_block(j, quadrant)
-                own = sums[j][rows, block * F_IN : (block + 1) * F_IN]
-                if quadrant % 2 == 0:
-                    nc.vector.tensor_copy(out=results[h][rows, r, :], in_=own)
-                else:
-                    nc.scalar.copy(out=results[h][rows, r, :], in_=own)
-                if r == HALF_TILES - 1:
-                    first = 8 * (quadrant // 2) + HALF_TILES * h
-                    nc.sync.dma_start(
-                        out=out[:, quadrant % 2, first : first + HALF_TILES, :].rearrange("n c f -> n (c f)"),
-                        in_=results[h][rows, :, :].rearrange("n r f -> n (r f)"),
-                    )
+                nc.sync.dma_start(
+                    out=out[:, quadrant % 2, 8 * (quadrant // 2) + j, :],
+                    in_=whole[rows, block * F_IN : (block + 1) * F_IN],
+                )
 
         units = [(rnd, g) for rnd in rounds for g in range(rnd["chunk"]["size"])]
         position = 0
@@ -225,7 +219,7 @@ def tile_dense_pa_k_kernel(tc, x, W_e, W_o, b, grad_out, out):
                     finish(job[0])
         while pieces:
             quantise(*pieces.pop(0)[1:])
-        for job in ready:
+        for job in sorted(ready, key=lambda job: job[0]):
             one_pass(*job)
             if job[1] == PASSES - 1:
                 finish(job[0])

@@ -14,39 +14,26 @@ ITEMS, PARITIES, COMPONENTS, DEGREES = 32, 2, 16, 4
 F_IN, F_OUT = 128, 8192
 
 P = 128
-K_PASS = 4 * P
-PASSES = F_OUT // K_PASS
+K_SLAB = 4 * P
+SLABS = F_OUT // K_SLAB
 MAX_CHUNK = 4
-HALF_TILES = 4
-N_MOVING = 4 * F_IN
-QUADRANT = 32
-PASS_WORDS = 2 * P
+HALF_ROWS = COMPONENTS * ITEMS
+W_COLS = PARITIES * 2 * F_IN
 
-HALVES = ((1, (1, 1, 2, 4, 4, 4)), (0, (4, 4, 4, 4)))
+PHASES = ((1, (1, 1, 2, 2, 2, 2, 2, 2, 2)), (0, (4, 4, 4, 4)))
 
-HEAD_RUN = 4
-HEAD_UNITS = 16
-RUN = 3
-BURST = 3
+RUN = (3, 3)
+PACE_LAG = 6
 LAG = 2
 PASS_LAG = 3
-COPY_MOD = 4
 
 RAW_BUFS = 8
-CODE_BUFS = 4
+GROUPED_G_BUFS = 5
+GROUPED_W_BUFS = 5
+W_CODE_BUFS = 9
 
 FLOPS = 2 * ITEMS * PARITIES * COMPONENTS * F_IN * F_OUT
 BYTES = 2 * (ITEMS * PARITIES * COMPONENTS + PARITIES * DEGREES * F_IN) * F_OUT + 4 * ITEMS * PARITIES * COMPONENTS * F_IN
-
-
-def window_of(j):
-    if j == 0:
-        return 0
-    return N_MOVING if j < HALF_TILES else N_MOVING // 2
-
-
-def own_block(j, quadrant):
-    return (quadrant + 2) % 4 if 0 < j < HALF_TILES else quadrant
 
 
 def tile_dense_pa_k_kernel(tc, x, W_e, W_o, b, grad_out, out):
@@ -54,172 +41,218 @@ def tile_dense_pa_k_kernel(tc, x, W_e, W_o, b, grad_out, out):
     with ExitStack() as ctx:
         const = ctx.enter_context(tc.tile_pool(name="const", bufs=1))
         raw_pool = ctx.enter_context(tc.tile_pool(name="raw", bufs=RAW_BUFS))
-        grouped_w_pool = ctx.enter_context(tc.tile_pool(name="grouped_w", bufs=2))
-        grouped_g_pool = ctx.enter_context(tc.tile_pool(name="grouped_g", bufs=3))
-        code_pool = ctx.enter_context(tc.tile_pool(name="grad_codes", bufs=CODE_BUFS))
-        result_pool = ctx.enter_context(tc.tile_pool(name="result", bufs=HALF_TILES))
+        grouped_w_pool = ctx.enter_context(tc.tile_pool(name="grouped_w", bufs=GROUPED_W_BUFS))
+        grouped_g_pool = ctx.enter_context(tc.tile_pool(name="grouped_g", bufs=GROUPED_G_BUFS))
+        w_code_pool = ctx.enter_context(tc.tile_pool(name="w_codes", bufs=W_CODE_BUFS))
+        result_pool = ctx.enter_context(tc.tile_pool(name="result", bufs=2))
         bank_pool = ctx.enter_context(tc.psum_pool(name="banks", bufs=4))
         sum_pool = ctx.enter_context(tc.psum_pool(name="sums", bufs=1))
         ctx.enter_context(tc.manual_schedule())
 
-        grad_rows = grad_out.flatten_outer_dims().rearrange("(q h v s) k -> h v q s k", h=2, v=2, s=2)
+        grad_rows = grad_out.flatten_outer_dims().rearrange("(q v s) k -> v q s k", v=4, s=2)
         weight_rows = [W.rearrange("(h l) f k -> h f l k", l=2) for W in (W_e, W_o)]
 
         identity = const.tile([P, P], F32, name="identity")
         make_identity(nc, identity[:])
         sorter = const.tile([P, P], F32, name="sorter")
         nc.vector.tensor_copy(
-            out=sorter[:].rearrange("i (x p n) -> i x p n", p=PARITIES, x=2),
-            in_=identity[:].rearrange("i (n p x) -> i x p n", p=PARITIES, x=2),
+            out=sorter[:].rearrange("i (y n) -> i y n", y=4),
+            in_=identity[:].rearrange("i (n y) -> i y n", y=4),
         )
 
-        weight_codes = const.tile([P, PASSES, 2 * N_MOVING], U32, name="weight_codes", align_bytes=64)
-        weight_scales = const.tile([P, PASSES, 2 * N_MOVING], U8, name="weight_scales", align_bytes=64)
+        grad_codes = const.tile([P, SLABS, 2 * HALF_ROWS], U32, name="grad_codes", align_bytes=64)
+        grad_scales = const.tile([P, SLABS, 2 * HALF_ROWS], U8, name="grad_scales", align_bytes=64)
 
-        chunks = []
-        for h, sizes in HALVES:
+        rounds = []
+        for h, sizes in PHASES:
             first = 0
             for size in sizes:
-                chunks.append({"h": h, "first": first, "size": size})
+                chunk = {"h": h, "first": first, "size": size, "grouped_w": {}, "grouped_g": {}}
+                for parity in range(PARITIES):
+                    rounds.append({"kind": "w", "chunk": chunk, "part": parity})
+                if h == 1:
+                    for v in range(4):
+                        rounds.append({"kind": "g", "chunk": chunk, "part": v})
                 first += size
-            assert first == PASSES
-
-        def weight_round(chunk, parity):
-            return {"grads": False, "chunk": chunk, "parity": parity}
-
-        rounds = [weight_round(chunks[0], 0), weight_round(chunks[0], 1)]
-        for i, chunk in enumerate(chunks):
-            for v in range(2):
-                rounds.append({"grads": True, "chunk": chunk, "v": v})
-                if i + 1 < len(chunks):
-                    rounds.append(weight_round(chunks[i + 1], v))
+            assert first == SLABS
 
         for rnd in rounds:
             chunk = rnd["chunk"]
-            width = chunk["size"] * K_PASS
-            k_cols = slice(chunk["first"] * K_PASS, chunk["first"] * K_PASS + width)
-            raw = raw_pool.tile([P, 2, MAX_CHUNK * K_PASS], BF16, name="raw")
-            if rnd["grads"]:
-                nc.sync.dma_start(out=raw[:, :, 0:width], in_=grad_rows[chunk["h"]][rnd["v"]][:, :, k_cols])
-            else:
-                nc.sync.dma_start(out=raw[:, :, 0:width], in_=weight_rows[rnd["parity"]][chunk["h"]][:, :, k_cols])
+            width = chunk["size"] * K_SLAB
+            k_cols = slice(chunk["first"] * K_SLAB, chunk["first"] * K_SLAB + width)
+            raw = raw_pool.tile([P, 2, MAX_CHUNK * K_SLAB], BF16, name="raw")
+            source = grad_rows[rnd["part"]] if rnd["kind"] == "g" else weight_rows[rnd["part"]][chunk["h"]]
+            nc.sync.dma_start(out=raw[:, :, 0:width], in_=source[:, :, k_cols])
             rnd["raw"] = raw
 
+        w_codes = {}
         sums = {}
         ready = []
-        counters = {"unit": 0}
         pieces = []
+        results = []
+        counters = {"unit": 0}
 
         def unit(rnd, g):
             chunk = rnd["chunk"]
-            if g == 0:
-                if rnd["grads"]:
-                    rnd["grouped"] = grouped_g_pool.tile([P, MAX_CHUNK * 2 * K_PASS], BF16, name="grouped_g", align_bytes=64)
-                elif rnd["parity"] == 0:
-                    chunk["grouped"] = grouped_w_pool.tile([P, MAX_CHUNK * 4 * K_PASS], BF16, name="grouped_w", align_bytes=64)
-            bank = bank_pool.tile([P, 2, 2, P], F32, name="bank")
-            for block in range(2):
-                raw_words = rnd["raw"][:, block, :].bitcast(F32)
-                for u in range(2):
-                    first = (2 * g + u) * P
-                    nc.tensor.transpose(bank[:, block, u, :], raw_words[:, first : first + P], sorter[:] if rnd["grads"] else identity[:])
-            if rnd["grads"]:
-                words = rnd["grouped"][:].bitcast(F32).rearrange("w (g s c u) -> w g s c u", g=MAX_CHUNK, s=2, u=2)
-                dst = words[:, g]
+            part = rnd["part"]
+            slab = chunk["first"] + g
+            raw = rnd["raw"]
+            if rnd["kind"] == "g":
+                if part == 0:
+                    chunk["grouped_g"][g] = grouped_g_pool.tile([P, 2 * HALF_ROWS * 4], BF16, name="grouped_g", align_bytes=64)
+                bank = bank_pool.tile([P, 2, 4, 2 * ITEMS], F32, name="bank")
+                for s in range(2):
+                    raw_words = raw[:, s, :].bitcast(F32)
+                    for u in range(2):
+                        first = (2 * g + u) * P
+                        nc.tensor.transpose(bank[:, u, :, s * ITEMS : (s + 1) * ITEMS], raw_words[:, first : first + P], sorter[:])
+                words = chunk["grouped_g"][g][:].bitcast(F32).rearrange("w (y c u) -> w y c u", y=4, u=2)
+                dst = words[:, :, part * 2 * ITEMS : (part + 1) * 2 * ITEMS, :]
+                src = bank[:].rearrange("w u y c -> w y c u")
+                on_vector = part < 3 and counters["unit"] % 2 == 0
             else:
-                words = chunk["grouped"][:].bitcast(F32).rearrange("w (g l p f u) -> w g l p f u", g=MAX_CHUNK, l=2, p=PARITIES, u=2)
-                dst = words[:, g, :, rnd["parity"]]
-            src = bank[:].rearrange("w s u c -> w s c u")
-            if counters["unit"] % COPY_MOD == 0:
+                if part == 0:
+                    chunk["grouped_w"][g] = grouped_w_pool.tile([P, W_COLS * 4], BF16, name="grouped_w", align_bytes=64)
+                bank = bank_pool.tile([P, 2, 2, P], F32, name="bank")
+                for l in range(2):
+                    raw_words = raw[:, l, :].bitcast(F32)
+                    for u in range(2):
+                        first = (2 * g + u) * P
+                        nc.tensor.transpose(bank[:, l, u, :], raw_words[:, first : first + P], identity[:])
+                words = chunk["grouped_w"][g][:].bitcast(F32).rearrange("w (p l f u) -> w p l f u", p=PARITIES, l=2, u=2)
+                dst = words[:, part]
+                src = bank[:].rearrange("w l u f -> w l f u")
+                on_vector = chunk["h"] == 0 and counters["unit"] % 4 == 0
+            if on_vector:
                 nc.vector.tensor_copy(out=dst, in_=src)
             else:
                 nc.scalar.copy(out=dst, in_=src)
             counters["unit"] += 1
-            size = chunk["size"]
-            if rnd["grads"]:
-                if g % 2 == 1 or g == size - 1:
-                    pieces.append((counters["unit"], rnd, g - g % 2, g + 1))
-            elif rnd["parity"] == 1:
-                pieces.append((counters["unit"], rnd, g, g + 1))
+            due = counters["unit"] + LAG
+            if rnd["kind"] == "g" and part == 3:
+                pieces.append((due, "g", chunk, g, 0))
+                pieces.append((due, "g", chunk, g, 1))
+            elif rnd["kind"] == "w" and part == 1:
+                pieces.append((due, "w", chunk, g, 0))
 
-        def quantise(rnd, g0, g1):
-            chunk = rnd["chunk"]
-            if rnd["grads"]:
-                if g0 == 0:
-                    rnd["codes"] = code_pool.tile([P, MAX_CHUNK * 2 * P], U32, name="grad_codes", align_bytes=64)
-                    rnd["scales"] = code_pool.tile([P, MAX_CHUNK * 2 * P], U8, name="grad_scales", align_bytes=64)
-                codes, scales = rnd["codes"], rnd["scales"]
-                nc.vector.quantize_mx(
-                    out=codes[:, g0 * 2 * P : g1 * 2 * P].bitcast(E5M2_X4),
-                    scales=scales[:, g0 * 2 * P : g1 * 2 * P],
-                    in_=rnd["grouped"][:, g0 * 2 * K_PASS : g1 * 2 * K_PASS],
-                )
-                for g in range(g0, g1):
-                    for s in range(2):
-                        rows = slice((2 * g + s) * P, (2 * g + s + 1) * P)
-                        ready.append((4 * chunk["h"] + 2 * rnd["v"] + s, chunk["first"] + g, codes[:, rows], scales[:, rows], counters["unit"]))
+        def quantise(kind, chunk, g, parity):
+            slab = chunk["first"] + g
+            if kind == "w":
+                codes = w_code_pool.tile([P, W_COLS], U32, name="w_codes", align_bytes=64)
+                scales = w_code_pool.tile([P, W_COLS], U8, name="w_scales", align_bytes=64)
+                nc.vector.quantize_mx(out=codes[:].bitcast(E4M3_X4), scales=scales[:], in_=chunk["grouped_w"][g][:])
+                w_codes[chunk["h"], slab] = (codes, scales)
+                if chunk["h"] == 0:
+                    for p in range(PARITIES):
+                        ready.append((counters["unit"] + PASS_LAG, 0, slab, p, 0))
             else:
-                grouped = chunk["grouped"]
-                for g in range(g0, g1):
-                    whole_pass = chunk["first"] + g
-                    if chunk["h"] == 1:
-                        parts = [(g * 4 * K_PASS, 4 * K_PASS, N_MOVING // 2)]
-                    else:
-                        parts = [(g * 4 * K_PASS, 2 * K_PASS, 0), (g * 4 * K_PASS + 2 * K_PASS, 2 * K_PASS, 3 * N_MOVING // 2)]
-                    for start, width, column in parts:
-                        nc.vector.quantize_mx(
-                            out=weight_codes[:, whole_pass, column : column + width // 4].bitcast(E4M3_X4),
-                            scales=weight_scales[:, whole_pass, column : column + width // 4],
-                            in_=grouped[:, start : start + width],
-                        )
+                cols = slice(parity * HALF_ROWS, (parity + 1) * HALF_ROWS)
+                nc.vector.quantize_mx(
+                    out=grad_codes[:, slab, cols].bitcast(E5M2_X4),
+                    scales=grad_scales[:, slab, cols],
+                    in_=chunk["grouped_g"][g][:, parity * 4 * HALF_ROWS : (parity + 1) * 4 * HALF_ROWS],
+                )
+                for l in range(2):
+                    ready.append((counters["unit"] + PASS_LAG, 1, slab, parity, l))
 
-        def one_pass(j, whole_pass, grad_codes, grad_scales, written):
-            if whole_pass == 0:
-                sums[j] = sum_pool.tile([P, N_MOVING], F32, name="sum%d" % (j % HALF_TILES))
-            columns = slice(window_of(j), window_of(j) + N_MOVING)
+        def one_pass(h, slab, parity, l):
+            codes, scales = w_codes[h, slab]
+            key = (h, parity, l)
+            if slab == 0:
+                tag = 2 * parity + l if h == 1 else parity
+                sums[key] = sum_pool.tile([P, HALF_ROWS], F32, name="sum%d" % tag)
+            if h == 1:
+                w_cols = slice((2 * parity + l) * F_IN, (2 * parity + l + 1) * F_IN)
+                g_cols = slice(parity * HALF_ROWS, (parity + 1) * HALF_ROWS)
+                lhsT, lhsT_scale = codes[:, w_cols].bitcast(E4M3_X4), scales[:, w_cols]
+                rhs, rhs_scale = grad_codes[:, slab, g_cols].bitcast(E5M2_X4), grad_scales[:, slab, g_cols]
+            else:
+                g_cols = slice(parity * HALF_ROWS, parity * HALF_ROWS + P)
+                lhsT, lhsT_scale = grad_codes[:, slab, g_cols].bitcast(E5M2_X4), grad_scales[:, slab, g_cols]
+                rhs, rhs_scale = codes[:].bitcast(E4M3_X4), scales[:]
             nc.tensor.matmul_mx(
-                out=sums[j][:],
-                lhsT=grad_codes.bitcast(E5M2_X4),
-                lhsT_scale=grad_scales,
-                rhs=weight_codes[:, whole_pass, columns].bitcast(E4M3_X4),
-                rhs_scale=weight_scales[:, whole_pass, columns],
-                start=(whole_pass == 0),
-                stop=(whole_pass == PASSES - 1),
+                out=sums[key][:],
+                lhsT=lhsT,
+                lhsT_scale=lhsT_scale,
+                rhs=rhs,
+                rhs_scale=rhs_scale,
+                start=(slab == 0),
+                stop=(slab == SLABS - 1),
             )
 
-        def finish(j):
-            whole = result_pool.tile([P, N_MOVING], F32, name="whole")
-            if j % 2 == 0:
-                nc.scalar.copy(out=whole[:], in_=sums[j][:])
+        def finish(h, parity, l):
+            if h == 1:
+                if l == 0:
+                    sums["turned", parity] = result_pool.tile([P, 12 * ITEMS], F32, name="turned")
+                turned = sums["turned", parity]
+                if l == 0:
+                    nc.vector.tensor_copy(out=turned[:, 0 : 5 * ITEMS], in_=sums[h, parity, l][:, 4 * ITEMS : 9 * ITEMS])
+                else:
+                    nc.scalar.copy(out=turned[:, 5 * ITEMS : 12 * ITEMS], in_=sums[h, parity, l][:, 9 * ITEMS : 16 * ITEMS])
+                    results.append((counters["unit"] + RUN[0], parity))
             else:
-                nc.vector.tensor_copy(out=whole[:], in_=sums[j][:])
-            for quadrant in range(4):
-                rows = slice(quadrant * QUADRANT, (quadrant + 1) * QUADRANT)
-                block = own_block(j, quadrant)
-                nc.sync.dma_start(
-                    out=out[:, quadrant % 2, 8 * (quadrant // 2) + j, :],
-                    in_=whole[rows, block * F_IN : (block + 1) * F_IN],
-                )
+                whole = result_pool.tile([P, 2 * F_IN], F32, name="whole")
+                src = sums[h, parity, l][:, parity * 2 * F_IN : (parity + 1) * 2 * F_IN]
+                if parity == 0:
+                    nc.scalar.copy(out=whole[:], in_=src)
+                else:
+                    nc.vector.tensor_copy(out=whole[:], in_=src)
+                for c in range(4):
+                    degree = min(c, 1)
+                    nc.sync.dma_start(
+                        out=out[:, parity, c, :],
+                        in_=whole[c * ITEMS : (c + 1) * ITEMS, degree * F_IN : (degree + 1) * F_IN],
+                    )
+
+        def turn_back(parity):
+            bank = bank_pool.tile([P, 3, P], F32, name="bank")
+            for i in range(3):
+                nc.tensor.transpose(bank[:, i, :], sums["turned", parity][:, i * P : (i + 1) * P], identity[:])
+            rows = result_pool.tile([P, 3, P], F32, name="rows")
+            nc.scalar.copy(out=rows[:], in_=bank[:])
+            for c in range(4):
+                nc.sync.dma_start(out=out[:, parity, 4 + c :: 4, :], in_=rows[c * ITEMS : (c + 1) * ITEMS, :, :])
 
         units = [(rnd, g) for rnd in rounds for g in range(rnd["chunk"]["size"])]
         position = 0
+        marks = []
+        for index, (rnd, g) in enumerate(units):
+            if g == 0 and rnd["part"] == (3 if rnd["chunk"]["h"] == 1 else 1) and rnd["kind"] == ("g" if rnd["chunk"]["h"] == 1 else "w"):
+                marks.append((index + 1, rnd["chunk"]["size"] * (4 if rnd["chunk"]["h"] == 1 else 2)))
+        marks.append((len(units), 0))
+
+        def planned(at):
+            total = 0.0
+            for (begin, passes), (end, ignored) in zip(marks, marks[1:]):
+                if at >= end:
+                    total += passes
+                elif at > begin:
+                    total += passes * (at - begin) / (end - begin)
+            return total
+
+        done = 0
         while position < len(units):
-            length = HEAD_RUN if position < HEAD_UNITS else RUN
-            for rnd, g in units[position : position + length]:
+            h = units[position][0]["chunk"]["h"]
+            while results and results[0][0] <= counters["unit"]:
+                turn_back(results.pop(0)[1])
+            for rnd, g in units[position : position + RUN[h]]:
                 unit(rnd, g)
-                while pieces and pieces[0][0] + LAG <= counters["unit"]:
+                if pieces and pieces[0][0] <= counters["unit"]:
                     quantise(*pieces.pop(0)[1:])
-            position += length
-            burst = [job for job in ready[: (HEAD_RUN if position <= HEAD_UNITS else BURST)] if job[4] + PASS_LAG <= counters["unit"]]
+            position += RUN[h]
+            wanted = max(0, round(planned(position - PACE_LAG)) - done)
+            burst = [job for job in ready[:wanted] if job[0] <= counters["unit"]]
+            burst = [job for job in burst if job[1] == burst[0][1]]
             ready = ready[len(burst) :]
+            done += len(burst)
             for job in burst:
-                one_pass(*job)
+                one_pass(*job[1:])
             for job in burst:
-                if job[1] == PASSES - 1:
-                    finish(job[0])
+                if job[2] == SLABS - 1:
+                    finish(job[1], job[3], job[4])
         while pieces:
             quantise(*pieces.pop(0)[1:])
-        for job in sorted(ready, key=lambda job: job[0]):
-            one_pass(*job)
-            if job[1] == PASSES - 1:
-                finish(job[0])
+        for job in sorted(ready, key=lambda job: job[3]):
+            one_pass(*job[1:])
+            if job[2] == SLABS - 1:
+                finish(job[1], job[3], job[4])

@@ -20,10 +20,15 @@ MAX_CHUNK = 4
 HALF_ROWS = COMPONENTS * ITEMS
 W_COLS = PARITIES * 2 * F_IN
 
-PHASES = ((1, (1, 1, 2, 2, 2, 2, 2, 2, 2)), (0, (4, 4, 4, 4)))
+SIZES = {
+    ("w", 1): ((1, 1, 2, 4, 4, 4), (1, 1, 2, 4, 4, 4)),
+    ("g", 1): ((1, 1, 2, 4, 4, 4), (1, 1, 3, 4, 4, 3), (1, 1, 4, 4, 4, 2), (1, 2, 4, 4, 4, 1)),
+    ("w", 0): ((4, 4, 4, 4), (4, 4, 4, 4)),
+    ("g", 0): (),
+}
 
 RUN = (3, 3)
-PACE_LAG = 6
+BURST = (3, 2)
 LAG = 2
 PASS_LAG = 3
 
@@ -64,27 +69,28 @@ def tile_dense_pa_k_kernel(tc, x, W_e, W_o, b, grad_out, out):
         grad_scales = const.tile([P, SLABS, 2 * HALF_ROWS], U8, name="grad_scales", align_bytes=64)
 
         rounds = []
-        for h, sizes in PHASES:
-            first = 0
-            for size in sizes:
-                chunk = {"h": h, "first": first, "size": size, "grouped_w": {}, "grouped_g": {}}
-                for parity in range(PARITIES):
-                    rounds.append({"kind": "w", "chunk": chunk, "part": parity})
-                if h == 1:
-                    for v in range(4):
-                        rounds.append({"kind": "g", "chunk": chunk, "part": v})
-                first += size
-            assert first == SLABS
+        for h in (1, 0):
+            sources = [[0, kind, part, list(sizes)] for kind in ("w", "g") for part, sizes in enumerate(SIZES[kind, h])]
+            while sources:
+                source = min(sources, key=lambda source: source[0])
+                first, kind, part, sizes = source
+                size = sizes.pop(0)
+                rounds.append({"h": h, "kind": kind, "part": part, "first": first, "size": size})
+                source[0] += size
+                if not sizes:
+                    assert source[0] == SLABS
+                    sources.remove(source)
 
         for rnd in rounds:
-            chunk = rnd["chunk"]
-            width = chunk["size"] * K_SLAB
-            k_cols = slice(chunk["first"] * K_SLAB, chunk["first"] * K_SLAB + width)
+            width = rnd["size"] * K_SLAB
+            k_cols = slice(rnd["first"] * K_SLAB, rnd["first"] * K_SLAB + width)
             raw = raw_pool.tile([P, 2, MAX_CHUNK * K_SLAB], BF16, name="raw")
-            source = grad_rows[rnd["part"]] if rnd["kind"] == "g" else weight_rows[rnd["part"]][chunk["h"]]
+            source = grad_rows[rnd["part"]] if rnd["kind"] == "g" else weight_rows[rnd["part"]][rnd["h"]]
             nc.sync.dma_start(out=raw[:, :, 0:width], in_=source[:, :, k_cols])
             rnd["raw"] = raw
 
+        grouped = {}
+        whole = {}
         w_codes = {}
         sums = {}
         ready = []
@@ -93,67 +99,73 @@ def tile_dense_pa_k_kernel(tc, x, W_e, W_o, b, grad_out, out):
         counters = {"unit": 0}
 
         def unit(rnd, g):
-            chunk = rnd["chunk"]
             part = rnd["part"]
-            slab = chunk["first"] + g
+            slab = rnd["first"] + g
             raw = rnd["raw"]
+            key = (rnd["kind"], rnd["h"], slab)
             if rnd["kind"] == "g":
-                if part == 0:
-                    chunk["grouped_g"][g] = grouped_g_pool.tile([P, 2 * HALF_ROWS * 4], BF16, name="grouped_g", align_bytes=64)
+                if key not in grouped:
+                    tile = grouped_g_pool.tile([P, 2 * HALF_ROWS * 4], BF16, name="grouped_g", align_bytes=64)
+                    grouped[key] = [tile, 4]
                 bank = bank_pool.tile([P, 2, 4, 2 * ITEMS], F32, name="bank")
                 for s in range(2):
                     raw_words = raw[:, s, :].bitcast(F32)
                     for u in range(2):
                         first = (2 * g + u) * P
                         nc.tensor.transpose(bank[:, u, :, s * ITEMS : (s + 1) * ITEMS], raw_words[:, first : first + P], sorter[:])
-                words = chunk["grouped_g"][g][:].bitcast(F32).rearrange("w (y c u) -> w y c u", y=4, u=2)
+                words = grouped[key][0][:].bitcast(F32).rearrange("w (y c u) -> w y c u", y=4, u=2)
                 dst = words[:, :, part * 2 * ITEMS : (part + 1) * 2 * ITEMS, :]
                 src = bank[:].rearrange("w u y c -> w y c u")
-                on_vector = part < 3 and counters["unit"] % 2 == 0
+                on_vector = counters["unit"] % 8 in (0, 3, 6)
             else:
-                if part == 0:
-                    chunk["grouped_w"][g] = grouped_w_pool.tile([P, W_COLS * 4], BF16, name="grouped_w", align_bytes=64)
+                if key not in grouped:
+                    tile = grouped_w_pool.tile([P, W_COLS * 4], BF16, name="grouped_w", align_bytes=64)
+                    grouped[key] = [tile, PARITIES]
                 bank = bank_pool.tile([P, 2, 2, P], F32, name="bank")
                 for l in range(2):
                     raw_words = raw[:, l, :].bitcast(F32)
                     for u in range(2):
                         first = (2 * g + u) * P
                         nc.tensor.transpose(bank[:, l, u, :], raw_words[:, first : first + P], identity[:])
-                words = chunk["grouped_w"][g][:].bitcast(F32).rearrange("w (p l f u) -> w p l f u", p=PARITIES, l=2, u=2)
+                words = grouped[key][0][:].bitcast(F32).rearrange("w (p l f u) -> w p l f u", p=PARITIES, l=2, u=2)
                 dst = words[:, part]
                 src = bank[:].rearrange("w l u f -> w l f u")
-                on_vector = chunk["h"] == 0 and counters["unit"] % 4 == 0
+                on_vector = rnd["h"] == 0 and counters["unit"] % 4 == 0
             if on_vector:
                 nc.vector.tensor_copy(out=dst, in_=src)
             else:
                 nc.scalar.copy(out=dst, in_=src)
             counters["unit"] += 1
             due = counters["unit"] + LAG
-            if rnd["kind"] == "g" and part == 3:
-                pieces.append((due, "g", chunk, g, 0))
-                pieces.append((due, "g", chunk, g, 1))
-            elif rnd["kind"] == "w" and part == 1:
-                pieces.append((due, "w", chunk, g, 0))
+            grouped[key][1] -= 1
+            if grouped[key][1] == 0:
+                for parity in range(PARITIES if rnd["kind"] == "g" else 1):
+                    pieces.append((due, key, parity))
 
-        def quantise(kind, chunk, g, parity):
-            slab = chunk["first"] + g
+        def quantise(key, parity):
+            kind, h, slab = key
+            tile = grouped[key][0]
             if kind == "w":
                 codes = w_code_pool.tile([P, W_COLS], U32, name="w_codes", align_bytes=64)
                 scales = w_code_pool.tile([P, W_COLS], U8, name="w_scales", align_bytes=64)
-                nc.vector.quantize_mx(out=codes[:].bitcast(E4M3_X4), scales=scales[:], in_=chunk["grouped_w"][g][:])
-                w_codes[chunk["h"], slab] = (codes, scales)
-                if chunk["h"] == 0:
-                    for p in range(PARITIES):
-                        ready.append((counters["unit"] + PASS_LAG, 0, slab, p, 0))
+                nc.vector.quantize_mx(out=codes[:].bitcast(E4M3_X4), scales=scales[:], in_=tile[:])
+                w_codes[h, slab] = (codes, scales)
             else:
                 cols = slice(parity * HALF_ROWS, (parity + 1) * HALF_ROWS)
                 nc.vector.quantize_mx(
                     out=grad_codes[:, slab, cols].bitcast(E5M2_X4),
                     scales=grad_scales[:, slab, cols],
-                    in_=chunk["grouped_g"][g][:, parity * 4 * HALF_ROWS : (parity + 1) * 4 * HALF_ROWS],
+                    in_=tile[:, parity * 4 * HALF_ROWS : (parity + 1) * 4 * HALF_ROWS],
                 )
-                for l in range(2):
-                    ready.append((counters["unit"] + PASS_LAG, 1, slab, parity, l))
+            if h == 0:
+                for p in range(PARITIES):
+                    ready.append((counters["unit"] + PASS_LAG, 0, slab, p, 0))
+            else:
+                whole[slab] = whole.get(slab, 0) + 1
+                if whole[slab] == 3:
+                    for p in range(PARITIES):
+                        for l in range(2):
+                            ready.append((counters["unit"] + PASS_LAG, 1, slab, p, l))
 
         def one_pass(h, slab, parity, l):
             codes, scales = w_codes[h, slab]
@@ -213,26 +225,10 @@ def tile_dense_pa_k_kernel(tc, x, W_e, W_o, b, grad_out, out):
             for c in range(4):
                 nc.sync.dma_start(out=out[:, parity, 4 + c :: 4, :], in_=rows[c * ITEMS : (c + 1) * ITEMS, :, :])
 
-        units = [(rnd, g) for rnd in rounds for g in range(rnd["chunk"]["size"])]
+        units = [(rnd, g) for rnd in rounds for g in range(rnd["size"])]
         position = 0
-        marks = []
-        for index, (rnd, g) in enumerate(units):
-            if g == 0 and rnd["part"] == (3 if rnd["chunk"]["h"] == 1 else 1) and rnd["kind"] == ("g" if rnd["chunk"]["h"] == 1 else "w"):
-                marks.append((index + 1, rnd["chunk"]["size"] * (4 if rnd["chunk"]["h"] == 1 else 2)))
-        marks.append((len(units), 0))
-
-        def planned(at):
-            total = 0.0
-            for (begin, passes), (end, ignored) in zip(marks, marks[1:]):
-                if at >= end:
-                    total += passes
-                elif at > begin:
-                    total += passes * (at - begin) / (end - begin)
-            return total
-
-        done = 0
         while position < len(units):
-            h = units[position][0]["chunk"]["h"]
+            h = units[position][0]["h"]
             while results and results[0][0] <= counters["unit"]:
                 turn_back(results.pop(0)[1])
             for rnd, g in units[position : position + RUN[h]]:
@@ -240,11 +236,9 @@ def tile_dense_pa_k_kernel(tc, x, W_e, W_o, b, grad_out, out):
                 if pieces and pieces[0][0] <= counters["unit"]:
                     quantise(*pieces.pop(0)[1:])
             position += RUN[h]
-            wanted = max(0, round(planned(position - PACE_LAG)) - done)
-            burst = [job for job in ready[:wanted] if job[0] <= counters["unit"]]
+            burst = [job for job in ready[: BURST[h]] if job[0] <= counters["unit"]]
             burst = [job for job in burst if job[1] == burst[0][1]]
             ready = ready[len(burst) :]
-            done += len(burst)
             for job in burst:
                 one_pass(*job[1:])
             for job in burst:

@@ -21,21 +21,23 @@ HALF_ROWS = COMPONENTS * ITEMS
 W_COLS = PARITIES * 2 * F_IN
 
 SIZES = {
-    ("w", 1): ((1, 1, 2, 4, 4, 4), (1, 1, 2, 4, 4, 4)),
-    ("g", 1): ((1, 1, 2, 4, 4, 4), (1, 1, 3, 4, 4, 3), (1, 1, 4, 4, 4, 2), (1, 2, 4, 4, 4, 1)),
+    ("w", 1): ((1, 1, 2, 4, 4, 4), (1, 1, 4, 4, 4, 2)),
+    ("g", 1): ((2, 4, 4, 4, 2), (1, 2, 4, 4, 4, 1), (1, 1, 3, 4, 4, 3), (1, 1, 2, 4, 4, 4)),
     ("w", 0): ((4, 4, 4, 4), (4, 4, 4, 4)),
     ("g", 0): (),
 }
 
-RUN = (3, 3)
-BURST = (3, 2)
+RUN = (4, 3)
+BURST = (4, 2)
 LAG = 2
+WARM_UNITS = (0, 0)
+WARM_MOD = (0,)
 PASS_LAG = 3
 
-RAW_BUFS = 8
-GROUPED_G_BUFS = 5
+RAW_BUFS = 7
+GROUPED_G_BUFS = 6
 GROUPED_W_BUFS = 5
-W_CODE_BUFS = 9
+W_CODE_BUFS = 10
 
 FLOPS = 2 * ITEMS * PARITIES * COMPONENTS * F_IN * F_OUT
 BYTES = 2 * (ITEMS * PARITIES * COMPONENTS + PARITIES * DEGREES * F_IN) * F_OUT + 4 * ITEMS * PARITIES * COMPONENTS * F_IN
@@ -98,6 +100,10 @@ def tile_dense_pa_k_kernel(tc, x, W_e, W_o, b, grad_out, out):
         results = []
         counters = {"unit": 0}
 
+        def keep_warm(bank):
+            if WARM_UNITS[0] <= counters["unit"] < WARM_UNITS[1] and counters["unit"] % 3 in WARM_MOD:
+                nc.tensor.matmul(bank[:, 0, 0, :], lhsT=identity[:], rhs=identity[:], start=True, stop=True)
+
         def unit(rnd, g):
             part = rnd["part"]
             slab = rnd["first"] + g
@@ -107,21 +113,23 @@ def tile_dense_pa_k_kernel(tc, x, W_e, W_o, b, grad_out, out):
                 if key not in grouped:
                     tile = grouped_g_pool.tile([P, 2 * HALF_ROWS * 4], BF16, name="grouped_g", align_bytes=64)
                     grouped[key] = [tile, 4]
-                bank = bank_pool.tile([P, 2, 4, 2 * ITEMS], F32, name="bank")
+                bank = bank_pool.tile([P, 2, 2, P], F32, name="bank")
+                keep_warm(bank)
                 for s in range(2):
                     raw_words = raw[:, s, :].bitcast(F32)
                     for u in range(2):
                         first = (2 * g + u) * P
-                        nc.tensor.transpose(bank[:, u, :, s * ITEMS : (s + 1) * ITEMS], raw_words[:, first : first + P], sorter[:])
-                words = grouped[key][0][:].bitcast(F32).rearrange("w (y c u) -> w y c u", y=4, u=2)
-                dst = words[:, :, part * 2 * ITEMS : (part + 1) * 2 * ITEMS, :]
-                src = bank[:].rearrange("w u y c -> w y c u")
+                        nc.tensor.transpose(bank[:, s, u, :], raw_words[:, first : first + P], sorter[:])
+                words = grouped[key][0][:].bitcast(F32).rearrange("w (y v s n u) -> w v y s n u", y=4, v=4, s=2, u=2)
+                dst = words[:, part]
+                src = bank[:].rearrange("w s u (y n) -> w y s n u", y=4)
                 on_vector = counters["unit"] % 8 in (0, 3, 6)
             else:
                 if key not in grouped:
                     tile = grouped_w_pool.tile([P, W_COLS * 4], BF16, name="grouped_w", align_bytes=64)
                     grouped[key] = [tile, PARITIES]
                 bank = bank_pool.tile([P, 2, 2, P], F32, name="bank")
+                keep_warm(bank)
                 for l in range(2):
                     raw_words = raw[:, l, :].bitcast(F32)
                     for u in range(2):

@@ -21,8 +21,8 @@ HALF_ROWS = COMPONENTS * ITEMS
 W_COLS = PARITIES * 2 * F_IN
 
 SIZES = {
-    ("w", 1): ((1, 1, 2, 4, 4, 4), (1, 1, 4, 4, 4, 2)),
-    ("g", 1): ((2, 4, 4, 4, 2), (1, 2, 4, 4, 4, 1), (1, 1, 3, 4, 4, 3), (1, 1, 2, 4, 4, 4)),
+    ("w", 1): ((1, 4, 4, 4, 3), (4, 4, 4, 4)),
+    ("g", 1): ((4, 4, 4, 4), (1, 4, 4, 4, 3), (2, 4, 4, 4, 2), (3, 4, 4, 4, 1)),
     ("w", 0): ((4, 4, 4, 4), (4, 4, 4, 4)),
     ("g", 0): (),
 }

@@ -67,8 +67,8 @@ def tile_dense_pa_k_kernel(tc, x, W_e, W_o, b, grad_out, out):
             in_=identity[:].rearrange("i (n y) -> i y n", y=4),
         )
 
-        grad_codes = const.tile([P, SLABS, 2 * HALF_ROWS], U32, name="grad_codes", align_bytes=64)
-        grad_scales = const.tile([P, SLABS, 2 * HALF_ROWS], U8, name="grad_scales", align_bytes=64)
+        grad_codes = const.tile([P, SLABS, 2 * HALF_ROWS], U32, name="grad_codes", align_bytes=256)
+        grad_scales = const.tile([P, SLABS, 2 * HALF_ROWS], U8, name="grad_scales", align_bytes=256)
 
         rounds = []
         for h in (1, 0):
@@ -98,7 +98,7 @@ def tile_dense_pa_k_kernel(tc, x, W_e, W_o, b, grad_out, out):
         ready = []
         pieces = []
         results = []
-        counters = {"unit": 0}
+        counters = {"unit": 0, "turned": 0}
 
         def keep_warm(bank):
             if WARM_UNITS[0] <= counters["unit"] < WARM_UNITS[1] and counters["unit"] % 3 in WARM_MOD:
@@ -123,12 +123,15 @@ def tile_dense_pa_k_kernel(tc, x, W_e, W_o, b, grad_out, out):
                 words = grouped[key][0][:].bitcast(F32).rearrange("w (y v s n u) -> w v y s n u", y=4, v=4, s=2, u=2)
                 dst = words[:, part]
                 src = bank[:].rearrange("w s u (y n) -> w y s n u", y=4)
-                on_vector = counters["unit"] % 8 in (0, 3, 6)
+                on_vector = counters["unit"] % 4 == 0
             else:
                 if key not in grouped:
                     tile = grouped_w_pool.tile([P, W_COLS * 4], BF16, name="grouped_w", align_bytes=64)
                     grouped[key] = [tile, PARITIES]
-                bank = bank_pool.tile([P, 2, 2, P], F32, name="bank")
+                if counters["turned"] == 4 and counters["unit"] % 6 >= 4:
+                    bank = sum_pool.tile([P, 2, 2, P], F32, name="sum%d" % (counters["unit"] % 6 - 2))
+                else:
+                    bank = bank_pool.tile([P, 2, 2, P], F32, name="bank")
                 keep_warm(bank)
                 for l in range(2):
                     raw_words = raw[:, l, :].bitcast(F32)
@@ -138,7 +141,7 @@ def tile_dense_pa_k_kernel(tc, x, W_e, W_o, b, grad_out, out):
                 words = grouped[key][0][:].bitcast(F32).rearrange("w (p l f u) -> w p l f u", p=PARITIES, l=2, u=2)
                 dst = words[:, part]
                 src = bank[:].rearrange("w l u f -> w l f u")
-                on_vector = rnd["h"] == 0 and counters["unit"] % 4 == 0
+                on_vector = counters["unit"] % 4 == 0
             if on_vector:
                 nc.vector.tensor_copy(out=dst, in_=src)
             else:
@@ -154,8 +157,8 @@ def tile_dense_pa_k_kernel(tc, x, W_e, W_o, b, grad_out, out):
             kind, h, slab = key
             tile = grouped[key][0]
             if kind == "w":
-                codes = w_code_pool.tile([P, W_COLS], U32, name="w_codes", align_bytes=64)
-                scales = w_code_pool.tile([P, W_COLS], U8, name="w_scales", align_bytes=64)
+                codes = w_code_pool.tile([P, W_COLS], U32, name="w_codes", align_bytes=256)
+                scales = w_code_pool.tile([P, W_COLS], U8, name="w_scales", align_bytes=256)
                 nc.vector.quantize_mx(out=codes[:].bitcast(E4M3_X4), scales=scales[:], in_=tile[:])
                 w_codes[h, slab] = (codes, scales)
             else:
@@ -201,6 +204,7 @@ def tile_dense_pa_k_kernel(tc, x, W_e, W_o, b, grad_out, out):
             )
 
         def finish(h, parity, l):
+            counters["turned"] += h
             if h == 1:
                 if l == 0:
                     sums["turned", parity] = result_pool.tile([P, 12 * ITEMS], F32, name="turned")
@@ -214,12 +218,13 @@ def tile_dense_pa_k_kernel(tc, x, W_e, W_o, b, grad_out, out):
                 whole = result_pool.tile([P, 2 * F_IN], F32, name="whole")
                 src = sums[h, parity, l][:, parity * 2 * F_IN : (parity + 1) * 2 * F_IN]
                 if parity == 0:
-                    nc.scalar.copy(out=whole[:], in_=src)
-                else:
                     nc.vector.tensor_copy(out=whole[:], in_=src)
+                else:
+                    nc.scalar.copy(out=whole[:], in_=src)
                 for c in range(4):
                     degree = min(c, 1)
-                    nc.sync.dma_start(
+                    queue = nc.scalar if parity == 1 and c >= 2 else nc.sync
+                    queue.dma_start(
                         out=out[:, parity, c, :],
                         in_=whole[c * ITEMS : (c + 1) * ITEMS, degree * F_IN : (degree + 1) * F_IN],
                     )

@@ -23,12 +23,12 @@ W_COLS = PARITIES * 2 * F_IN
 SIZES = {
     ("w", 1): ((1, 4, 4, 4, 3), (4, 4, 4, 4)),
     ("g", 1): ((4, 4, 4, 4), (1, 4, 4, 4, 3), (2, 4, 4, 4, 2), (3, 4, 4, 4, 1)),
-    ("w", 0): ((4, 4, 4, 4), (4, 4, 4, 4)),
+    ("w", 0): ((4, 4, 4, 2, 2), (4, 4, 4, 2, 2)),
     ("g", 0): (),
 }
 
-RUN = (4, 3)
-BURST = (4, 2)
+RUN = (4, 4)
+BURST = (4, 3)
 LAG = 2
 WARM_UNITS = (0, 0)
 WARM_MOD = (0,)

@@ -21,9 +21,9 @@ HALF_ROWS = COMPONENTS * ITEMS
 W_COLS = PARITIES * 2 * F_IN
 
 SIZES = {
-    ("w", 1): ((1, 4, 4, 4, 3), (4, 4, 4, 4)),
+    ("w", 1): ((1, 4, 4, 4, 3), (3, 4, 4, 4, 1)),
     ("g", 1): ((4, 4, 4, 4), (1, 4, 4, 4, 3), (2, 4, 4, 4, 2), (3, 4, 4, 4, 1)),
-    ("w", 0): ((4, 4, 4, 2, 2), (4, 4, 4, 2, 2)),
+    ("w", 0): ((2, 2, 2, 2, 2, 2, 2, 2), (2, 2, 2, 2, 2, 2, 2, 2)),
     ("g", 0): (),
 }
 
@@ -123,7 +123,7 @@ def tile_dense_pa_k_kernel(tc, x, W_e, W_o, b, grad_out, out):
                 words = grouped[key][0][:].bitcast(F32).rearrange("w (y v s n u) -> w v y s n u", y=4, v=4, s=2, u=2)
                 dst = words[:, part]
                 src = bank[:].rearrange("w s u (y n) -> w y s n u", y=4)
-                on_vector = counters["unit"] % 4 == 0
+                on_vector = counters["unit"] % 5 == 0
             else:
                 if key not in grouped:
                     tile = grouped_w_pool.tile([P, W_COLS * 4], BF16, name="grouped_w", align_bytes=64)
@@ -141,7 +141,7 @@ def tile_dense_pa_k_kernel(tc, x, W_e, W_o, b, grad_out, out):
                 words = grouped[key][0][:].bitcast(F32).rearrange("w (p l f u) -> w p l f u", p=PARITIES, l=2, u=2)
                 dst = words[:, part]
                 src = bank[:].rearrange("w l u f -> w l f u")
-                on_vector = counters["unit"] % 4 == 0
+                on_vector = counters["unit"] % 5 == 0
             if on_vector:
                 nc.vector.tensor_copy(out=dst, in_=src)
             else:

from contextlib import ExitStack

import concourse.mybir as mybir
from concourse.masks import make_identity

F32 = mybir.dt.float32
BF16 = mybir.dt.bfloat16
U32 = mybir.dt.uint32
U8 = mybir.dt.uint8
E4M3_X4 = mybir.dt.float8_e4m3fn_x4
E5M2_X4 = mybir.dt.float8_e5m2_x4

ITEMS, PARITIES, COMPONENTS, DEGREES = 32, 2, 16, 4
F_IN, F_OUT = 128, 8192

P = 128
K_SLAB = 4 * P
SLABS = F_OUT // K_SLAB
MAX_CHUNK = 4
HALF_ROWS = COMPONENTS * ITEMS
W_COLS = PARITIES * 2 * F_IN

SIZES = {
    ("w", 1): ((1, 4, 4, 4, 3), (3, 4, 4, 4, 1)),
    ("g", 1): ((4, 4, 4, 4), (1, 4, 4, 4, 3), (2, 4, 4, 4, 2), (3, 4, 4, 4, 1)),
    ("w", 0): ((2, 2, 2, 2, 2, 2, 2, 2), (2, 2, 2, 2, 2, 2, 2, 2)),
    ("g", 0): (),
}

RUN = (4, 4)
BURST = (4, 3)
LAG = 2
WARM_UNITS = (0, 0)
WARM_MOD = (0,)
PASS_LAG = 3

RAW_BUFS = 7
GROUPED_G_BUFS = 6
GROUPED_W_BUFS = 5
W_CODE_BUFS = 10

FLOPS = 2 * ITEMS * PARITIES * COMPONENTS * F_IN * F_OUT
BYTES = 2 * (ITEMS * PARITIES * COMPONENTS + PARITIES * DEGREES * F_IN) * F_OUT + 4 * ITEMS * PARITIES * COMPONENTS * F_IN


def tile_dense_pa_k_kernel(tc, x, W_e, W_o, b, grad_out, out):
    nc = tc.nc
    with ExitStack() as ctx:
        const = ctx.enter_context(tc.tile_pool(name="const", bufs=1))
        raw_pool = ctx.enter_context(tc.tile_pool(name="raw", bufs=RAW_BUFS))
        grouped_w_pool = ctx.enter_context(tc.tile_pool(name="grouped_w", bufs=GROUPED_W_BUFS))
        grouped_g_pool = ctx.enter_context(tc.tile_pool(name="grouped_g", bufs=GROUPED_G_BUFS))
        w_code_pool = ctx.enter_context(tc.tile_pool(name="w_codes", bufs=W_CODE_BUFS))
        result_pool = ctx.enter_context(tc.tile_pool(name="result", bufs=2))
        bank_pool = ctx.enter_context(tc.psum_pool(name="banks", bufs=4))
        sum_pool = ctx.enter_context(tc.psum_pool(name="sums", bufs=1))
        ctx.enter_context(tc.manual_schedule())

        grad_rows = grad_out.flatten_outer_dims().rearrange("(q v s) k -> v q s k", v=4, s=2)
        weight_rows = [W.rearrange("(h l) f k -> h f l k", l=2) for W in (W_e, W_o)]

        identity = const.tile([P, P], F32, name="identity")
        make_identity(nc, identity[:])
        sorter = const.tile([P, P], F32, name="sorter")
        nc.vector.tensor_copy(
            out=sorter[:].rearrange("i (y n) -> i y n", y=4),
            in_=identity[:].rearrange("i (n y) -> i y n", y=4),
        )

        grad_codes = const.tile([P, SLABS, 2 * HALF_ROWS], U32, name="grad_codes", align_bytes=256)
        grad_scales = const.tile([P, SLABS, 2 * HALF_ROWS], U8, name="grad_scales", align_bytes=256)

        rounds = []
        for h in (1, 0):
            sources = [[0, kind, part, list(sizes)] for kind in ("w", "g") for part, sizes in enumerate(SIZES[kind, h])]
            while sources:
                source = min(sources, key=lambda source: source[0])
                first, kind, part, sizes = source
                size = sizes.pop(0)
                rounds.append({"h": h, "kind": kind, "part": part, "first": first, "size": size})
                source[0] += size
                if not sizes:
                    assert source[0] == SLABS
                    sources.remove(source)

        for rnd in rounds:
            width = rnd["size"] * K_SLAB
            k_cols = slice(rnd["first"] * K_SLAB, rnd["first"] * K_SLAB + width)
            raw = raw_pool.tile([P, 2, MAX_CHUNK * K_SLAB], BF16, name="raw")
            source = grad_rows[rnd["part"]] if rnd["kind"] == "g" else weight_rows[rnd["part"]][rnd["h"]]
            nc.sync.dma_start(out=raw[:, :, 0:width], in_=source[:, :, k_cols])
            rnd["raw"] = raw

        grouped = {}
        whole = {}
        w_codes = {}
        sums = {}
        ready = []
        pieces = []
        results = []
        counters = {"unit": 0, "turned": 0}

        def keep_warm(bank):
            if WARM_UNITS[0] <= counters["unit"] < WARM_UNITS[1] and counters["unit"] % 3 in WARM_MOD:
                nc.tensor.matmul(bank[:, 0, 0, :], lhsT=identity[:], rhs=identity[:], start=True, stop=True)

        def unit(rnd, g):
            part = rnd["part"]
            slab = rnd["first"] + g
            raw = rnd["raw"]
            key = (rnd["kind"], rnd["h"], slab)
            if rnd["kind"] == "g":
                if key not in grouped:
                    tile = grouped_g_pool.tile([P, 2 * HALF_ROWS * 4], BF16, name="grouped_g", align_bytes=64)
                    grouped[key] = [tile, 4]
                bank = bank_pool.tile([P, 2, 2, P], F32, name="bank")
                keep_warm(bank)
                for s in range(2):
                    raw_words = raw[:, s, :].bitcast(F32)
                    for u in range(2):
                        first = (2 * g + u) * P
                        nc.tensor.transpose(bank[:, s, u, :], raw_words[:, first : first + P], sorter[:])
                words = grouped[key][0][:].bitcast(F32).rearrange("w (y v s n u) -> w v y s n u", y=4, v=4, s=2, u=2)
                dst = words[:, part]
                src = bank[:].rearrange("w s u (y n) -> w y s n u", y=4)
                on_vector = counters["unit"] % 5 == 0
            else:
                if key not in grouped:
                    tile = grouped_w_pool.tile([P, W_COLS * 4], BF16, name="grouped_w", align_bytes=64)
                    grouped[key] = [tile, PARITIES]
                if counters["turned"] == 4 and counters["unit"] % 6 >= 4:
                    bank = sum_pool.tile([P, 2, 2, P], F32, name="sum%d" % (counters["unit"] % 6 - 2))
                else:
                    bank = bank_pool.tile([P, 2, 2, P], F32, name="bank")
                keep_warm(bank)
                for l in range(2):
                    raw_words = raw[:, l, :].bitcast(F32)
                    for u in range(2):
                        first = (2 * g + u) * P
                        nc.tensor.transpose(bank[:, l, u, :], raw_words[:, first : first + P], identity[:])
                words = grouped[key][0][:].bitcast(F32).rearrange("w (p l f u) -> w p l f u", p=PARITIES, l=2, u=2)
                dst = words[:, part]
                src = bank[:].rearrange("w l u f -> w l f u")
                on_vector = counters["unit"] % 5 == 0
            if on_vector:
                nc.vector.tensor_copy(out=dst, in_=src)
            else:
                nc.scalar.copy(out=dst, in_=src)
            counters["unit"] += 1
            due = counters["unit"] + LAG
            grouped[key][1] -= 1
            if grouped[key][1] == 0:
                for parity in range(PARITIES if rnd["kind"] == "g" else 1):
                    pieces.append((due, key, parity))

        def quantise(key, parity):
            kind, h, slab = key
            tile = grouped[key][0]
            if kind == "w":
                codes = w_code_pool.tile([P, W_COLS], U32, name="w_codes", align_bytes=256)
                scales = w_code_pool.tile([P, W_COLS], U8, name="w_scales", align_bytes=256)
                nc.vector.quantize_mx(out=codes[:].bitcast(E4M3_X4), scales=scales[:], in_=tile[:])
                w_codes[h, slab] = (codes, scales)
            else:
                cols = slice(parity * HALF_ROWS, (parity + 1) * HALF_ROWS)
                nc.vector.quantize_mx(
                    out=grad_codes[:, slab, cols].bitcast(E5M2_X4),
                    scales=grad_scales[:, slab, cols],
                    in_=tile[:, parity * 4 * HALF_ROWS : (parity + 1) * 4 * HALF_ROWS],
                )
            if h == 0:
                for p in range(PARITIES):
                    ready.append((counters["unit"] + PASS_LAG, 0, slab, p, 0))
            else:
                whole[slab] = whole.get(slab, 0) + 1
                if whole[slab] == 3:
                    for p in range(PARITIES):
                        for l in range(2):
                            ready.append((counters["unit"] + PASS_LAG, 1, slab, p, l))

        def one_pass(h, slab, parity, l):
            codes, scales = w_codes[h, slab]
            key = (h, parity, l)
            if slab == 0:
                tag = 2 * parity + l if h == 1 else parity
                sums[key] = sum_pool.tile([P, HALF_ROWS], F32, name="sum%d" % tag)
            if h == 1:
                w_cols = slice((2 * parity + l) * F_IN, (2 * parity + l + 1) * F_IN)
                g_cols = slice(parity * HALF_ROWS, (parity + 1) * HALF_ROWS)
                lhsT, lhsT_scale = codes[:, w_cols].bitcast(E4M3_X4), scales[:, w_cols]
                rhs, rhs_scale = grad_codes[:, slab, g_cols].bitcast(E5M2_X4), grad_scales[:, slab, g_cols]
            else:
                g_cols = slice(parity * HALF_ROWS, parity * HALF_ROWS + P)
                lhsT, lhsT_scale = grad_codes[:, slab, g_cols].bitcast(E5M2_X4), grad_scales[:, slab, g_cols]
                rhs, rhs_scale = codes[:].bitcast(E4M3_X4), scales[:]
            nc.tensor.matmul_mx(
                out=sums[key][:],
                lhsT=lhsT,
                lhsT_scale=lhsT_scale,
                rhs=rhs,
                rhs_scale=rhs_scale,
                start=(slab == 0),
                stop=(slab == SLABS - 1),
            )

        def finish(h, parity, l):
            counters["turned"] += h
            if h == 1:
                if l == 0:
                    sums["turned", parity] = result_pool.tile([P, 12 * ITEMS], F32, name="turned")
                turned = sums["turned", parity]
                if l == 0:
                    nc.vector.tensor_copy(out=turned[:, 0 : 5 * ITEMS], in_=sums[h, parity, l][:, 4 * ITEMS : 9 * ITEMS])
                else:
                    nc.scalar.copy(out=turned[:, 5 * ITEMS : 12 * ITEMS], in_=sums[h, parity, l][:, 9 * ITEMS : 16 * ITEMS])
                    results.append((counters["unit"] + RUN[0], parity))
            else:
                whole = result_pool.tile([P, 2 * F_IN], F32, name="whole")
                src = sums[h, parity, l][:, parity * 2 * F_IN : (parity + 1) * 2 * F_IN]
                if parity == 0:
                    nc.vector.tensor_copy(out=whole[:], in_=src)
                else:
                    nc.scalar.copy(out=whole[:], in_=src)
                for c in range(4):
                    degree = min(c, 1)
                    queue = nc.scalar if parity == 1 and c >= 2 else nc.sync
                    queue.dma_start(
                        out=out[:, parity, c, :],
                        in_=whole[c * ITEMS : (c + 1) * ITEMS, degree * F_IN : (degree + 1) * F_IN],
                    )

        def turn_back(parity):
            bank = bank_pool.tile([P, 3, P], F32, name="bank")
            for i in range(3):
                nc.tensor.transpose(bank[:, i, :], sums["turned", parity][:, i * P : (i + 1) * P], identity[:])
            rows = result_pool.tile([P, 3, P], F32, name="rows")
            nc.scalar.copy(out=rows[:], in_=bank[:])
            for c in range(4):
                nc.sync.dma_start(out=out[:, parity, 4 + c :: 4, :], in_=rows[c * ITEMS : (c + 1) * ITEMS, :, :])

        units = [(rnd, g) for rnd in rounds for g in range(rnd["size"])]
        position = 0
        while position < len(units):
            h = units[position][0]["h"]
            while results and results[0][0] <= counters["unit"]:
                turn_back(results.pop(0)[1])
            for rnd, g in units[position : position + RUN[h]]:
                unit(rnd, g)
                if pieces and pieces[0][0] <= counters["unit"]:
                    quantise(*pieces.pop(0)[1:])
            position += RUN[h]
            burst = [job for job in ready[: BURST[h]] if job[0] <= counters["unit"]]
            burst = [job for job in burst if job[1] == burst[0][1]]
            ready = ready[len(burst) :]
            for job in burst:
                one_pass(*job[1:])
            for job in burst:
                if job[2] == SLABS - 1:
                    finish(job[1], job[3], job[4])
        while pieces:
            quantise(*pieces.pop(0)[1:])
        for job in sorted(ready, key=lambda job: job[3]):
            one_pass(*job[1:])
            if job[2] == SLABS - 1:
                finish(job[1], job[3], job[4])
